import numpy as np
import ml_dtypes


def mxq(x, axis, fmt="e4m3"):
    dtype, down = {"e4m3": (ml_dtypes.float8_e4m3fn, 7), "e5m2": (ml_dtypes.float8_e5m2, 14)}[fmt]
    v = np.moveaxis(np.asarray(x, np.float32).astype(ml_dtypes.bfloat16).astype(np.float64), axis, -1)
    blocks = v.reshape(v.shape[:-1] + (-1, 32))
    amax = np.abs(blocks).max(-1, keepdims=True)
    byte = np.maximum(np.where(amax > 0, np.frexp(amax)[1] - 1 + 127, 0) - down, 1)
    scale = np.exp2(byte - 127.0)
    codes = (blocks / scale).astype(np.float32).astype(dtype).astype(np.float64)
    return np.moveaxis((codes * scale).reshape(v.shape), -1, axis)


WIDE = False


def mx_kscale(k):
    if not WIDE:
        return np.ones(k)
    levels = np.array([10, -10, 5, -5, 0])
    a = np.random.permutation(np.resize(levels, k // 512 * 4)).reshape(k // 512, 4)
    idx = np.arange(k)
    return np.exp2(a[idx // 512, idx % 128 // 32])


BF16 = ml_dtypes.bfloat16


def bf(x):
    return np.asarray(x, np.float32).astype(BF16)


def f64(x):
    return np.asarray(x).astype(np.float64)


B, N, C, H = 2, 1024, 128, 2
HD = C // H
ALPHA = 0.6
SIG = 2.0


def get_s(w):
    d = w.sum(-1) ** -0.5
    return np.swapaxes(w, -1, -2) * d[..., :, None] * d[..., None, :]


def merge(o):
    return o.transpose(0, 2, 1, 3).reshape(B, N, C)


def draw_map(t):
    e = np.exp(SIG * np.random.standard_normal((B, H, N, N))) * t
    rows = np.exp(0.5 * np.random.standard_normal((B, H, N, 1)))
    return bf(e / e.sum(-1, keepdims=True) * rows)


def setup_inputs():
    t = mx_kscale(N)
    t = t / t.max()
    return {"attn_r": draw_map(t), "attn_d": draw_map(t),
            "v_d": bf(np.random.standard_normal((B, H, N, HD)) * 1.4 / t[:, None])}


def reference(attn_r, attn_d, v_d):
    wr, wd, v = f64(attn_r), f64(attn_d), f64(v_d)
    sr = mxq(get_s(wr), 3, "e4m3")
    sd = mxq(get_s(wd), 3, "e4m3")
    p = sr @ sd.transpose(0, 1, 3, 2)
    a = ALPHA * p + (1.0 - ALPHA) * (wr + wd)
    vq = mxq(v, 2, "e4m3")
    out_rd = merge(mxq(a, 3, "e4m3") @ vq)
    out_d = merge(mxq(wd, 3, "e4m3") @ vq)
    return (out_rd, out_d)

@@ -1,0 +1,295 @@
+from contextlib import ExitStack
+
+import concourse.mybir as mybir
+from concourse.masks import make_identity
+
+F32 = mybir.dt.float32
+BF16 = mybir.dt.bfloat16
+U32 = mybir.dt.uint32
+U8 = mybir.dt.uint8
+FP8X4 = mybir.dt.float8_e4m3fn_x4
+ALU = mybir.AluOpType
+ACT = mybir.ActivationFunctionType
+
+B, H, N, HD = 2, 2, 1024, 64
+ALPHA = 0.6
+BETA = 1.0 - ALPHA
+
+P = 128
+PACK = 4
+K_PASS = P * PACK
+PASSES = N // K_PASS
+ROW_TILES = N // P
+BANK = 512
+LOAD_TILES = 2
+GROUP_COLS = 512
+CHUNK = 2
+SUM_BUFS = 11
+
+FLOPS = B * H * (2 * N * N * N + 2 * (2 * N * N * HD))
+
+
+def row_tiles(flat):
+    return flat.rearrange("p (r j) -> p r j", r=ROW_TILES)
+
+
+def tile_multiattention_pa_t_kernel(tc, attn_r, attn_d, v_d, out_rd, out_d):
+    nc = tc.nc
+    with ExitStack() as ctx:
+        consts = ctx.enter_context(tc.tile_pool(name="consts", bufs=1))
+        maps = ctx.enter_context(tc.tile_pool(name="maps", bufs=2))
+        sums = ctx.enter_context(tc.tile_pool(name="sums", bufs=SUM_BUFS))
+        small = ctx.enter_context(tc.tile_pool(name="small", bufs=2))
+        spread = ctx.enter_context(tc.tile_pool(name="spread", bufs=1))
+        planes_pool = ctx.enter_context(tc.tile_pool(name="planes", bufs=2))
+        stage = ctx.enter_context(tc.tile_pool(name="stage", bufs=3))
+        keep = ctx.enter_context(tc.tile_pool(name="keep", bufs=1))
+        outs = ctx.enter_context(tc.tile_pool(name="outs", bufs=2))
+        p_psum = ctx.enter_context(tc.psum_pool(name="p_psum", bufs=4))
+        t_psum = ctx.enter_context(tc.psum_pool(name="t_psum", bufs=2))
+        o_psum = ctx.enter_context(tc.psum_pool(name="o_psum", bufs=2))
+
+        ident_f32 = consts.tile([P, P], F32)
+        make_identity(nc, ident_f32[:])
+        ident_bf16 = consts.tile([P, P], BF16)
+        make_identity(nc, ident_bf16[:])
+        minus_half = consts.tile([P, ROW_TILES], F32)
+        nc.vector.memset(minus_half[:], -0.5)
+
+        sr_codes = keep.tile([P, PASSES, N], U32, align_bytes=64)
+        sr_scales = keep.tile([P, PASSES, N], U8, align_bytes=64)
+        sd_codes = keep.tile([P, PASSES, N], U32, align_bytes=64)
+        sd_scales = keep.tile([P, PASSES, N], U8, align_bytes=64)
+
+        def load_maps(b, h):
+            w_r = maps.tile([P, ROW_TILES * N], BF16)
+            w_d = maps.tile([P, ROW_TILES * N], BF16)
+            src_r = attn_r[b, h].rearrange("(r p) j -> p r j", p=P)
+            src_d = attn_d[b, h].rearrange("(r p) j -> p r j", p=P)
+            for r0 in range(0, ROW_TILES, LOAD_TILES):
+                some = slice(r0, r0 + LOAD_TILES)
+                nc.sync.dma_start(out=row_tiles(w_d[:])[:, some, :], in_=src_d[:, some, :])
+                nc.sync.dma_start(out=row_tiles(w_r[:])[:, some, :], in_=src_r[:, some, :])
+            acc_d = small.tile([P, ROW_TILES], F32)
+            acc_u = small.tile([P, ROW_TILES], F32)
+            return {"b": b, "h": h, "w_r": w_r, "w_d": w_d, "acc_d": acc_d, "acc_u": acc_u, "u": []}
+
+        def add_maps_and_sum_rows(head, r):
+            u = sums.tile([P, N], F32)
+            nc.scalar.activation(
+                out=u[:],
+                in_=row_tiles(head["w_d"][:])[:, r, :],
+                func=ACT.Copy,
+                scale=BETA,
+                accum_out=head["acc_d"][:, r : r + 1],
+            )
+            nc.vector.scalar_tensor_tensor(
+                out=u[:],
+                in0=row_tiles(head["w_r"][:])[:, r, :],
+                scalar=BETA,
+                in1=u[:],
+                op0=ALU.mult,
+                op1=ALU.add,
+                accum_out=head["acc_u"][:, r : r + 1],
+            )
+            head["u"].append(u)
+
+        def spread_along_rows(factor, factor_row):
+            for half in range(N // BANK):
+                row_ps = t_psum.tile([P, BANK // P, P], F32, tag="t_ps")
+                for a in range(BANK // P):
+                    r = half * (BANK // P) + a
+                    nc.tensor.transpose(
+                        out=row_ps[:, a, :],
+                        in_=factor[:, r : r + 1].to_broadcast([P, P]),
+                        identity=ident_f32[:],
+                    )
+                nc.scalar.copy(
+                    out=factor_row[:, half * BANK : (half + 1) * BANK],
+                    in_=row_ps[:].rearrange("p a j -> p (a j)"),
+                )
+
+        def quantise_s(w, factor, factor_row, codes, scales):
+            for c in range(PASSES):
+                planes = planes_pool.tile([P, PACK, N], BF16)
+                for t in range(PACK):
+                    r = PACK * c + t
+                    nc.vector.scalar_tensor_tensor(
+                        out=planes[:, t, :],
+                        in0=row_tiles(w[:])[:, r, :],
+                        scalar=factor[:, r : r + 1],
+                        in1=factor_row[:],
+                        op0=ALU.mult,
+                        op1=ALU.mult,
+                    )
+                for n0 in range(0, N, GROUP_COLS):
+                    cols = slice(n0, n0 + GROUP_COLS)
+                    grouped = stage.tile([P, GROUP_COLS, PACK], BF16, align_bytes=64)
+                    nc.scalar.copy(
+                        out=grouped[:].rearrange("p (a i) t -> p a t i", i=4),
+                        in_=planes[:, :, cols].rearrange("p t (a i) -> p a t i", i=4),
+                    )
+                    nc.vector.quantize_mx(
+                        out=codes[:, c, cols].bitcast(FP8X4),
+                        scales=scales[:, c, cols],
+                        in_=grouped[:].rearrange("p n t -> p (n t)"),
+                    )
+
+        def fused_map_rows(head, r):
+            rows = slice(r * P, (r + 1) * P)
+            a_rows = stage.tile([P, N], BF16)
+            for m0 in range(0, N, BANK):
+                cols = slice(m0, m0 + BANK)
+                p_ps = p_psum.tile([P, BANK], F32)
+                for c in range(PASSES):
+                    nc.tensor.matmul_mx(
+                        out=p_ps[:],
+                        lhsT=sr_codes[:, c, rows].bitcast(FP8X4),
+                        lhsT_scale=sr_scales[:, c, rows],
+                        rhs=sd_codes[:, c, cols].bitcast(FP8X4),
+                        rhs_scale=sd_scales[:, c, cols],
+                        start=(c == 0),
+                        stop=(c == PASSES - 1),
+                    )
+                nc.vector.scalar_tensor_tensor(
+                    out=a_rows[:, cols],
+                    in0=p_ps[:],
+                    scalar=ALPHA,
+                    in1=head["u"][r][:, cols],
+                    op0=ALU.mult,
+                    op1=ALU.add,
+                )
+            return a_rows
+
+        def flip_computed_rows(a_rows, flipped, slot):
+            t_ps = t_psum.tile([P, PASSES, PACK, P], BF16, tag="t_ps")
+            every_second = a_rows[:].rearrange("i (g u q e) -> i g u e q", g=PASSES, u=2, e=2)
+            for g in range(PASSES):
+                for u in range(2):
+                    for e in range(2):
+                        nc.tensor.transpose(
+                            out=t_ps[:, g, 2 * u + e, :],
+                            in_=every_second[:, g, u, e, :],
+                            identity=ident_bf16[:],
+                        )
+            nc.scalar.copy(
+                out=flipped[:].rearrange("q (g i t) -> q g i t", g=PASSES, t=PACK)[
+                    :, :, slot * P : (slot + 1) * P, :
+                ],
+                in_=t_ps[:].rearrange("q g t i -> q g i t"),
+            )
+
+        def flip_input_rows(w, r, flipped, slot):
+            t_ps = t_psum.tile([P, PASSES * 2, P], F32, tag="t_ps")
+            words = w[:].bitcast(F32).rearrange("i (r x) -> i r x", r=ROW_TILES)
+            for gu in range(PASSES * 2):
+                nc.tensor.transpose(
+                    out=t_ps[:, gu, :],
+                    in_=words[:, r, gu * P : (gu + 1) * P],
+                    identity=ident_f32[:],
+                )
+            nc.scalar.copy(
+                out=flipped[:].bitcast(F32).rearrange("q (g i u) -> q g i u", g=PASSES, u=2)[
+                    :, :, slot * P : (slot + 1) * P, :
+                ],
+                in_=t_ps[:].rearrange("q (g u) i -> q g i u", u=2),
+            )
+
+        def times_values(flipped, head, r0, o_sb, out):
+            b, h = head["b"], head["h"]
+            f_codes = stage.tile([P, PASSES * CHUNK * P], U32, align_bytes=64)
+            f_scales = stage.tile([P, PASSES * CHUNK * P], U8, align_bytes=64)
+            nc.vector.quantize_mx(out=f_codes[:].bitcast(FP8X4), scales=f_scales[:], in_=flipped[:])
+            o_ps = o_psum.tile([P, CHUNK, P], F32)
+            for slot in range(CHUNK):
+                for g in range(PASSES):
+                    rows = slice((g * CHUNK + slot) * P, (g * CHUNK + slot + 1) * P)
+                    vals = slice((b * PASSES + g) * H * HD, (b * PASSES + g + 1) * H * HD)
+                    nc.tensor.matmul_mx(
+                        out=o_ps[:, slot, :],
+                        lhsT=f_codes[:, rows].bitcast(FP8X4),
+                        lhsT_scale=f_scales[:, rows],
+                        rhs=v_codes[:, vals].bitcast(FP8X4),
+                        rhs_scale=v_scales[:, vals],
+                        start=(g == 0),
+                        stop=(g == PASSES - 1),
+                    )
+            mine = slice(h * HD, (h + 1) * HD)
+            some = slice(r0, r0 + CHUNK)
+            nc.scalar.copy(out=o_sb[:, some, mine], in_=o_ps[:, :, mine])
+            if h == H - 1:
+                nc.sync.dma_start(
+                    out=out[b].rearrange("(r p) c -> p r c", p=P)[:, some, :], in_=o_sb[:, some, :]
+                )
+
+        heads = [load_maps(0, 0), load_maps(0, 1)]
+
+        v_rows = consts.tile([P, B * H * N * HD // P], BF16)
+        nc.sync.dma_start(
+            out=v_rows[:].rearrange("q (x y) -> q x y", y=2 * HD),
+            in_=v_d.rearrange("b h (g u q e) d -> q (b h g u) (e d)", g=PASSES, u=2, q=P, e=2),
+        )
+        v_grouped = consts.tile([P, B * H * N * HD // P], BF16, align_bytes=64)
+        v_from = v_rows[:].rearrange(
+            "q (b h g u e d) -> q b g h d (u e)", b=B, h=H, g=PASSES, u=2, e=2
+        )
+        v_to = v_grouped[:].rearrange("q (b g h d t) -> q b g h d t", b=B, g=PASSES, h=H, t=PACK)
+        for b in range(B):
+            for g in range(PASSES):
+                nc.vector.tensor_copy(out=v_to[:, b, g], in_=v_from[:, b, g])
+        v_codes = consts.tile([P, B * PASSES * H * HD], U32, align_bytes=64)
+        v_scales = consts.tile([P, B * PASSES * H * HD], U8, align_bytes=64)
+        nc.vector.quantize_mx(out=v_codes[:].bitcast(FP8X4), scales=v_scales[:], in_=v_grouped[:])
+
+        for r in range(ROW_TILES):
+            add_maps_and_sum_rows(heads[0], r)
+
+        o_rd = None
+        o_d = None
+        for i in range(B * H):
+            head = heads[i]
+
+            sum_d = small.tile([P, ROW_TILES], F32)
+            nc.vector.tensor_scalar_mul(out=sum_d[:], in0=head["acc_d"][:], scalar1=1.0 / BETA)
+            dd = small.tile([P, ROW_TILES], F32)
+            nc.gpsimd.tensor_tensor(out=dd[:], in0=sum_d[:], in1=minus_half[:], op=ALU.pow)
+            dd_row = spread.tile([P, N], F32)
+            spread_along_rows(dd, dd_row)
+            quantise_s(head["w_d"], dd, dd_row, sd_codes, sd_scales)
+
+            sum_r = small.tile([P, ROW_TILES], F32)
+            nc.vector.scalar_tensor_tensor(
+                out=sum_r[:],
+                in0=head["acc_u"][:],
+                scalar=1.0 / BETA,
+                in1=sum_d[:],
+                op0=ALU.mult,
+                op1=ALU.subtract,
+            )
+            dr = small.tile([P, ROW_TILES], F32)
+            nc.gpsimd.tensor_tensor(out=dr[:], in0=sum_r[:], in1=minus_half[:], op=ALU.pow)
+            dr_row = spread.tile([P, N], F32)
+            spread_along_rows(dr, dr_row)
+            quantise_s(head["w_r"], dr, dr_row, sr_codes, sr_scales)
+
+            if head["h"] == 0:
+                o_rd = outs.tile([P, ROW_TILES, H * HD], F32)
+                o_d = outs.tile([P, ROW_TILES, H * HD], F32)
+
+            for r0 in range(0, ROW_TILES, CHUNK):
+                flipped = stage.tile([P, PASSES * CHUNK * P * PACK], BF16, align_bytes=64)
+                for slot in range(CHUNK):
+                    flip_input_rows(head["w_d"], r0 + slot, flipped, slot)
+                times_values(flipped, head, r0, o_d, out_d)
+
+            if i + 2 < B * H:
+                heads.append(load_maps((i + 2) // H, (i + 2) % H))
+
+            for r0 in range(0, ROW_TILES, CHUNK):
+                flipped = stage.tile([P, PASSES * CHUNK * P * PACK], BF16, align_bytes=64)
+                for slot in range(CHUNK):
+                    if i + 1 < B * H:
+                        add_maps_and_sum_rows(heads[i + 1], r0 + slot)
+                    a_rows = fused_map_rows(head, r0 + slot)
+                    flip_computed_rows(a_rows, flipped, slot)
+                times_values(flipped, head, r0, o_rd, out_rd)

@@ -21,10 +21,17 @@ K_PASS = P * PACK
 PASSES = N // K_PASS
 ROW_TILES = N // P
 BANK = 512
+HALVES = N // BANK
 LOAD_TILES = 2
-GROUP_COLS = 512
 CHUNK = 2
-SUM_BUFS = 11
+UT_BUFS = PASSES * (ROW_TILES + 2)
+SUM_BUFS = 5
+
+ROUNDS = 2 * ROW_TILES
+T_LOAD = 0
+T_S = T_LOAD + ROUNDS + ROW_TILES
+T_A = T_S + ROW_TILES
+T_SUMS = T_A - ROUNDS - 2
 
 FLOPS = B * H * (2 * N * N * N + 2 * (2 * N * N * HD))
 
@@ -39,20 +46,18 @@ def tile_multiattention_pa_t_kernel(tc, attn_r, attn_d, v_d, out_rd, out_d):
         consts = ctx.enter_context(tc.tile_pool(name="consts", bufs=1))
         maps = ctx.enter_context(tc.tile_pool(name="maps", bufs=2))
         sums = ctx.enter_context(tc.tile_pool(name="sums", bufs=SUM_BUFS))
+        flipped_sums = ctx.enter_context(tc.tile_pool(name="flipped_sums", bufs=UT_BUFS))
         small = ctx.enter_context(tc.tile_pool(name="small", bufs=2))
-        spread = ctx.enter_context(tc.tile_pool(name="spread", bufs=1))
-        planes_pool = ctx.enter_context(tc.tile_pool(name="planes", bufs=2))
+        planes_pool = ctx.enter_context(tc.tile_pool(name="planes", bufs=4))
         stage = ctx.enter_context(tc.tile_pool(name="stage", bufs=3))
         keep = ctx.enter_context(tc.tile_pool(name="keep", bufs=1))
-        outs = ctx.enter_context(tc.tile_pool(name="outs", bufs=2))
+        outs = ctx.enter_context(tc.tile_pool(name="outs", bufs=1))
         p_psum = ctx.enter_context(tc.psum_pool(name="p_psum", bufs=4))
         t_psum = ctx.enter_context(tc.psum_pool(name="t_psum", bufs=2))
         o_psum = ctx.enter_context(tc.psum_pool(name="o_psum", bufs=2))
 
-        ident_f32 = consts.tile([P, P], F32)
-        make_identity(nc, ident_f32[:])
-        ident_bf16 = consts.tile([P, P], BF16)
-        make_identity(nc, ident_bf16[:])
+        ident = consts.tile([P, P], F32)
+        make_identity(nc, ident[:])
         minus_half = consts.tile([P, ROW_TILES], F32)
         nc.vector.memset(minus_half[:], -0.5)
 
@@ -60,8 +65,14 @@ def tile_multiattention_pa_t_kernel(tc, attn_r, attn_d, v_d, out_rd, out_d):
         sr_scales = keep.tile([P, PASSES, N], U8, align_bytes=64)
         sd_codes = keep.tile([P, PASSES, N], U32, align_bytes=64)
         sd_scales = keep.tile([P, PASSES, N], U8, align_bytes=64)
+        s_codes = {"r": sr_codes, "d": sd_codes}
+        s_scales = {"r": sr_scales, "d": sd_scales}
 
-        def load_maps(b, h):
+        o_rd = [outs.tile([P, ROW_TILES, H * HD], F32, name="o_rd%d" % b) for b in range(B)]
+        o_d = [outs.tile([P, ROW_TILES, H * HD], F32, name="o_d%d" % b) for b in range(B)]
+
+        def load_maps(head, r):
+            b, h = head["b"], head["h"]
             w_r = maps.tile([P, ROW_TILES * N], BF16)
             w_d = maps.tile([P, ROW_TILES * N], BF16)
             src_r = attn_r[b, h].rearrange("(r p) j -> p r j", p=P)
@@ -72,9 +83,9 @@ def tile_multiattention_pa_t_kernel(tc, attn_r, attn_d, v_d, out_rd, out_d):
                 nc.sync.dma_start(out=row_tiles(w_r[:])[:, some, :], in_=src_r[:, some, :])
             acc_d = small.tile([P, ROW_TILES], F32)
             acc_u = small.tile([P, ROW_TILES], F32)
-            return {"b": b, "h": h, "w_r": w_r, "w_d": w_d, "acc_d": acc_d, "acc_u": acc_u, "u": []}
+            head["w_r"], head["w_d"], head["acc_d"], head["acc_u"] = w_r, w_d, acc_d, acc_u
 
-        def add_maps_and_sum_rows(head, r):
+        def scale_d(head, r):
             u = sums.tile([P, N], F32)
             nc.scalar.activation(
                 out=u[:],
@@ -83,6 +94,10 @@ def tile_multiattention_pa_t_kernel(tc, attn_r, attn_d, v_d, out_rd, out_d):
                 scale=BETA,
                 accum_out=head["acc_d"][:, r : r + 1],
             )
+            head["u"].append(u)
+
+        def add_r(head, r):
+            u = head["u"][r]
             nc.vector.scalar_tensor_tensor(
                 out=u[:],
                 in0=row_tiles(head["w_r"][:])[:, r, :],
@@ -92,204 +107,230 @@ def tile_multiattention_pa_t_kernel(tc, attn_r, attn_d, v_d, out_rd, out_d):
                 op1=ALU.add,
                 accum_out=head["acc_u"][:, r : r + 1],
             )
-            head["u"].append(u)
 
-        def spread_along_rows(factor, factor_row):
-            for half in range(N // BANK):
-                row_ps = t_psum.tile([P, BANK // P, P], F32, tag="t_ps")
-                for a in range(BANK // P):
-                    r = half * (BANK // P) + a
-                    nc.tensor.transpose(
-                        out=row_ps[:, a, :],
-                        in_=factor[:, r : r + 1].to_broadcast([P, P]),
-                        identity=ident_f32[:],
-                    )
-                nc.scalar.copy(
-                    out=factor_row[:, half * BANK : (half + 1) * BANK],
-                    in_=row_ps[:].rearrange("p a j -> p (a j)"),
-                )
-
-        def quantise_s(w, factor, factor_row, codes, scales):
-            for c in range(PASSES):
-                planes = planes_pool.tile([P, PACK, N], BF16)
+        def flip_sum(head, r):
+            u = head["u"][r]
+            for g in range(PASSES):
+                ut_ps = t_psum.tile([P, PACK, P], F32, tag="t_ps")
                 for t in range(PACK):
-                    r = PACK * c + t
-                    nc.vector.scalar_tensor_tensor(
-                        out=planes[:, t, :],
-                        in0=row_tiles(w[:])[:, r, :],
-                        scalar=factor[:, r : r + 1],
-                        in1=factor_row[:],
-                        op0=ALU.mult,
-                        op1=ALU.mult,
-                    )
-                for n0 in range(0, N, GROUP_COLS):
-                    cols = slice(n0, n0 + GROUP_COLS)
-                    grouped = stage.tile([P, GROUP_COLS, PACK], BF16, align_bytes=64)
-                    nc.scalar.copy(
-                        out=grouped[:].rearrange("p (a i) t -> p a t i", i=4),
-                        in_=planes[:, :, cols].rearrange("p t (a i) -> p a t i", i=4),
-                    )
-                    nc.vector.quantize_mx(
-                        out=codes[:, c, cols].bitcast(FP8X4),
-                        scales=scales[:, c, cols],
-                        in_=grouped[:].rearrange("p n t -> p (n t)"),
-                    )
+                    m0 = g * K_PASS + t * P
+                    nc.tensor.transpose(out=ut_ps[:, t, :], in_=u[:, m0 : m0 + P], identity=ident[:])
+                ut = flipped_sums.tile([P, P, PACK], F32)
+                nc.scalar.copy(out=ut[:], in_=ut_ps[:].rearrange("q t i -> q i t"))
+                head["ut"].append(ut)
 
-        def fused_map_rows(head, r):
-            rows = slice(r * P, (r + 1) * P)
-            a_rows = stage.tile([P, N], BF16)
-            for m0 in range(0, N, BANK):
-                cols = slice(m0, m0 + BANK)
-                p_ps = p_psum.tile([P, BANK], F32)
-                for c in range(PASSES):
-                    nc.tensor.matmul_mx(
-                        out=p_ps[:],
-                        lhsT=sr_codes[:, c, rows].bitcast(FP8X4),
-                        lhsT_scale=sr_scales[:, c, rows],
-                        rhs=sd_codes[:, c, cols].bitcast(FP8X4),
-                        rhs_scale=sd_scales[:, c, cols],
-                        start=(c == 0),
-                        stop=(c == PASSES - 1),
-                    )
-                nc.vector.scalar_tensor_tensor(
-                    out=a_rows[:, cols],
-                    in0=p_ps[:],
-                    scalar=ALPHA,
-                    in1=head["u"][r][:, cols],
-                    op0=ALU.mult,
-                    op1=ALU.add,
-                )
-            return a_rows
-
-        def flip_computed_rows(a_rows, flipped, slot):
-            t_ps = t_psum.tile([P, PASSES, PACK, P], BF16, tag="t_ps")
-            every_second = a_rows[:].rearrange("i (g u q e) -> i g u e q", g=PASSES, u=2, e=2)
-            for g in range(PASSES):
-                for u in range(2):
-                    for e in range(2):
-                        nc.tensor.transpose(
-                            out=t_ps[:, g, 2 * u + e, :],
-                            in_=every_second[:, g, u, e, :],
-                            identity=ident_bf16[:],
-                        )
-            nc.scalar.copy(
-                out=flipped[:].rearrange("q (g i t) -> q g i t", g=PASSES, t=PACK)[
-                    :, :, slot * P : (slot + 1) * P, :
-                ],
-                in_=t_ps[:].rearrange("q g t i -> q g i t"),
-            )
-
-        def flip_input_rows(w, r, flipped, slot):
-            t_ps = t_psum.tile([P, PASSES * 2, P], F32, tag="t_ps")
-            words = w[:].bitcast(F32).rearrange("i (r x) -> i r x", r=ROW_TILES)
-            for gu in range(PASSES * 2):
-                nc.tensor.transpose(
-                    out=t_ps[:, gu, :],
-                    in_=words[:, r, gu * P : (gu + 1) * P],
-                    identity=ident_f32[:],
-                )
-            nc.scalar.copy(
-                out=flipped[:].bitcast(F32).rearrange("q (g i u) -> q g i u", g=PASSES, u=2)[
-                    :, :, slot * P : (slot + 1) * P, :
-                ],
-                in_=t_ps[:].rearrange("q (g u) i -> q g i u", u=2),
-            )
-
-        def times_values(flipped, head, r0, o_sb, out):
-            b, h = head["b"], head["h"]
-            f_codes = stage.tile([P, PASSES * CHUNK * P], U32, align_bytes=64)
-            f_scales = stage.tile([P, PASSES * CHUNK * P], U8, align_bytes=64)
-            nc.vector.quantize_mx(out=f_codes[:].bitcast(FP8X4), scales=f_scales[:], in_=flipped[:])
-            o_ps = o_psum.tile([P, CHUNK, P], F32)
-            for slot in range(CHUNK):
-                for g in range(PASSES):
-                    rows = slice((g * CHUNK + slot) * P, (g * CHUNK + slot + 1) * P)
-                    vals = slice((b * PASSES + g) * H * HD, (b * PASSES + g + 1) * H * HD)
-                    nc.tensor.matmul_mx(
-                        out=o_ps[:, slot, :],
-                        lhsT=f_codes[:, rows].bitcast(FP8X4),
-                        lhsT_scale=f_scales[:, rows],
-                        rhs=v_codes[:, vals].bitcast(FP8X4),
-                        rhs_scale=v_scales[:, vals],
-                        start=(g == 0),
-                        stop=(g == PASSES - 1),
-                    )
-            mine = slice(h * HD, (h + 1) * HD)
-            some = slice(r0, r0 + CHUNK)
-            nc.scalar.copy(out=o_sb[:, some, mine], in_=o_ps[:, :, mine])
-            if h == H - 1:
-                nc.sync.dma_start(
-                    out=out[b].rearrange("(r p) c -> p r c", p=P)[:, some, :], in_=o_sb[:, some, :]
-                )
-
-        heads = [load_maps(0, 0), load_maps(0, 1)]
-
-        v_rows = consts.tile([P, B * H * N * HD // P], BF16)
-        nc.sync.dma_start(
-            out=v_rows[:].rearrange("q (x y) -> q x y", y=2 * HD),
-            in_=v_d.rearrange("b h (g u q e) d -> q (b h g u) (e d)", g=PASSES, u=2, q=P, e=2),
-        )
-        v_grouped = consts.tile([P, B * H * N * HD // P], BF16, align_bytes=64)
-        v_from = v_rows[:].rearrange(
-            "q (b h g u e d) -> q b g h d (u e)", b=B, h=H, g=PASSES, u=2, e=2
-        )
-        v_to = v_grouped[:].rearrange("q (b g h d t) -> q b g h d t", b=B, g=PASSES, h=H, t=PACK)
-        for b in range(B):
-            for g in range(PASSES):
-                nc.vector.tensor_copy(out=v_to[:, b, g], in_=v_from[:, b, g])
-        v_codes = consts.tile([P, B * PASSES * H * HD], U32, align_bytes=64)
-        v_scales = consts.tile([P, B * PASSES * H * HD], U8, align_bytes=64)
-        nc.vector.quantize_mx(out=v_codes[:].bitcast(FP8X4), scales=v_scales[:], in_=v_grouped[:])
-
-        for r in range(ROW_TILES):
-            add_maps_and_sum_rows(heads[0], r)
-
-        o_rd = None
-        o_d = None
-        for i in range(B * H):
-            head = heads[i]
-
+        def root_d(head):
             sum_d = small.tile([P, ROW_TILES], F32)
             nc.vector.tensor_scalar_mul(out=sum_d[:], in0=head["acc_d"][:], scalar1=1.0 / BETA)
             dd = small.tile([P, ROW_TILES], F32)
             nc.gpsimd.tensor_tensor(out=dd[:], in0=sum_d[:], in1=minus_half[:], op=ALU.pow)
-            dd_row = spread.tile([P, N], F32)
-            spread_along_rows(dd, dd_row)
-            quantise_s(head["w_d"], dd, dd_row, sd_codes, sd_scales)
+            head["sum_d"], head["d"] = sum_d, dd
 
+        def root_r(head):
             sum_r = small.tile([P, ROW_TILES], F32)
             nc.vector.scalar_tensor_tensor(
                 out=sum_r[:],
                 in0=head["acc_u"][:],
                 scalar=1.0 / BETA,
-                in1=sum_d[:],
+                in1=head["sum_d"][:],
                 op0=ALU.mult,
                 op1=ALU.subtract,
             )
             dr = small.tile([P, ROW_TILES], F32)
             nc.gpsimd.tensor_tensor(out=dr[:], in0=sum_r[:], in1=minus_half[:], op=ALU.pow)
-            dr_row = spread.tile([P, N], F32)
-            spread_along_rows(dr, dr_row)
-            quantise_s(head["w_r"], dr, dr_row, sr_codes, sr_scales)
+            head["r"] = dr
 
-            if head["h"] == 0:
-                o_rd = outs.tile([P, ROW_TILES, H * HD], F32)
-                o_d = outs.tile([P, ROW_TILES, H * HD], F32)
+        def piece(j):
+            return "dr"[j // (HALVES * PASSES)], (j // PASSES) % HALVES, j % PASSES
 
-            for r0 in range(0, ROW_TILES, CHUNK):
+        def spread_factors(head, j):
+            which, half, c = piece(j)
+            if c == 0:
+                row = p_psum.tile([P, BANK // P, P], F32, tag="p_ps")
+                for a in range(BANK // P):
+                    r = half * (BANK // P) + a
+                    nc.tensor.transpose(
+                        out=row[:, a, :],
+                        in_=head[which][:, r : r + 1].to_broadcast([P, P]),
+                        identity=ident[:],
+                    )
+                head["rows"].append(row)
+
+        def scale_planes(head, j):
+            which, half, c = piece(j)
+            cols = slice(half * BANK, (half + 1) * BANK)
+            planes = planes_pool.tile([P, PACK, BANK], BF16)
+            for t in range(PACK):
+                r = PACK * c + t
+                nc.vector.scalar_tensor_tensor(
+                    out=planes[:, t, :],
+                    in0=row_tiles(head["w_" + which][:])[:, r, cols],
+                    scalar=head[which][:, r : r + 1],
+                    in1=head["rows"][j // PASSES][:].rearrange("p a x -> p (a x)"),
+                    op0=ALU.mult,
+                    op1=ALU.mult,
+                )
+            head["planes"].append(planes)
+
+        def regroup(head, j):
+            grouped = stage.tile([P, BANK, PACK], BF16, align_bytes=64)
+            nc.scalar.copy(
+                out=grouped[:].rearrange("p (a i) t -> p a t i", i=4),
+                in_=head["planes"][j][:].rearrange("p t (a i) -> p a t i", i=4),
+            )
+            head["grouped"].append(grouped)
+
+        def quantise_s(head, j):
+            which, half, c = piece(j)
+            cols = slice(half * BANK, (half + 1) * BANK)
+            nc.vector.quantize_mx(
+                out=s_codes[which][:, c, cols].bitcast(FP8X4),
+                scales=s_scales[which][:, c, cols],
+                in_=head["grouped"][j][:].rearrange("p n t -> p (n t)"),
+            )
+
+        def products(head, r):
+            rows = slice(r * P, (r + 1) * P)
+            for g in range(PASSES):
+                pt_ps = p_psum.tile([P, PACK, P], F32, tag="p_ps")
+                for t in range(PACK):
+                    cols = slice(g * K_PASS + t * P, g * K_PASS + (t + 1) * P)
+                    for c in range(PASSES):
+                        nc.tensor.matmul_mx(
+                            out=pt_ps[:, t, :],
+                            lhsT=s_codes["d"][:, c, cols].bitcast(FP8X4),
+                            lhsT_scale=s_scales["d"][:, c, cols],
+                            rhs=s_codes["r"][:, c, rows].bitcast(FP8X4),
+                            rhs_scale=s_scales["r"][:, c, rows],
+                            start=(c == 0),
+                            stop=(c == PASSES - 1),
+                        )
+                head["pt"].append(pt_ps)
+
+        def new_flipped(head, key, r):
+            if r % CHUNK == 0:
                 flipped = stage.tile([P, PASSES * CHUNK * P * PACK], BF16, align_bytes=64)
-                for slot in range(CHUNK):
-                    flip_input_rows(head["w_d"], r0 + slot, flipped, slot)
-                times_values(flipped, head, r0, o_d, out_d)
+                head[key] = flipped
+            return head[key], r % CHUNK
 
-            if i + 2 < B * H:
-                heads.append(load_maps((i + 2) // H, (i + 2) % H))
+        def finish_a(head, r):
+            flipped, slot = new_flipped(head, "a_flipped", r)
+            for g in range(PASSES):
+                nc.vector.scalar_tensor_tensor(
+                    out=flipped[:].rearrange("q (g i t) -> q g i t", g=PASSES, t=PACK)[
+                        :, g, slot * P : (slot + 1) * P, :
+                    ],
+                    in0=head["pt"][PASSES * r + g][:].rearrange("q t i -> q i t"),
+                    scalar=ALPHA,
+                    in1=head["ut"][PASSES * r + g][:],
+                    op0=ALU.mult,
+                    op1=ALU.add,
+                )
 
-            for r0 in range(0, ROW_TILES, CHUNK):
-                flipped = stage.tile([P, PASSES * CHUNK * P * PACK], BF16, align_bytes=64)
+        def flip_d(head, r):
+            t_ps = t_psum.tile([P, PASSES * 2, P], F32, tag="t_ps")
+            words = head["w_d"][:].bitcast(F32).rearrange("i (r x) -> i r x", r=ROW_TILES)
+            for gu in range(PASSES * 2):
+                nc.tensor.transpose(
+                    out=t_ps[:, gu, :], in_=words[:, r, gu * P : (gu + 1) * P], identity=ident[:]
+                )
+            head["dt_ps"].append(t_ps)
+
+        def copy_flipped_d(head, r):
+            flipped, slot = new_flipped(head, "d_flipped", r)
+            nc.scalar.copy(
+                out=flipped[:].bitcast(F32).rearrange("q (g i u) -> q g i u", g=PASSES, u=2)[
+                    :, :, slot * P : (slot + 1) * P, :
+                ],
+                in_=head["dt_ps"][r][:].rearrange("q (g u) i -> q g i u", u=2),
+            )
+
+        def quantise_flipped(head, key, r):
+            if r % CHUNK == CHUNK - 1:
+                f_codes = stage.tile([P, PASSES * CHUNK * P], U32, align_bytes=64)
+                f_scales = stage.tile([P, PASSES * CHUNK * P], U8, align_bytes=64)
+                nc.vector.quantize_mx(
+                    out=f_codes[:].bitcast(FP8X4), scales=f_scales[:], in_=head[key + "_flipped"][:]
+                )
+                head[key + "_mx"].append((f_codes, f_scales))
+
+        def times_values(head, key, r, values, o_sb, out):
+            if r % CHUNK == CHUNK - 1:
+                b, h = head["b"], head["h"]
+                f_codes, f_scales = head[key + "_mx"][r // CHUNK]
+                v_codes, v_scales = values
+                o_ps = o_psum.tile([P, CHUNK, P], F32)
                 for slot in range(CHUNK):
-                    if i + 1 < B * H:
-                        add_maps_and_sum_rows(heads[i + 1], r0 + slot)
-                    a_rows = fused_map_rows(head, r0 + slot)
-                    flip_computed_rows(a_rows, flipped, slot)
-                times_values(flipped, head, r0, o_rd, out_rd)
+                    for g in range(PASSES):
+                        rows = slice((g * CHUNK + slot) * P, (g * CHUNK + slot + 1) * P)
+                        vals = slice((b * PASSES + g) * H * HD, (b * PASSES + g + 1) * H * HD)
+                        nc.tensor.matmul_mx(
+                            out=o_ps[:, slot, :],
+                            lhsT=f_codes[:, rows].bitcast(FP8X4),
+                            lhsT_scale=f_scales[:, rows],
+                            rhs=v_codes[:, vals].bitcast(FP8X4),
+                            rhs_scale=v_scales[:, vals],
+                            start=(g == 0),
+                            stop=(g == PASSES - 1),
+                        )
+                mine = slice(h * HD, (h + 1) * HD)
+                some = slice(r + 1 - CHUNK, r + 1)
+                nc.scalar.copy(out=o_sb[b][:, some, mine], in_=o_ps[:, :, mine])
+                if h == H - 1:
+                    nc.sync.dma_start(
+                        out=out[b].rearrange("(r p) c -> p r c", p=P)[:, some, :], in_=o_sb[b][:, some, :]
+                    )
+
+        def quantise_values(which, rows_of_v):
+            v_rows = stage.tile([P, B * H * N * HD // P], BF16, tag="flipped", align_bytes=64)
+            nc.scalar.dma_start(
+                out=v_rows[:].rearrange("q (x y) -> q x y", x=rows_of_v.shape[1]), in_=rows_of_v
+            )
+            v_grouped = stage.tile([P, B * H * N * HD // P], BF16, tag="flipped", align_bytes=64)
+            v_from = v_rows[:].rearrange("q (b h g t d) -> q b g h d t", b=B, h=H, g=PASSES, t=PACK)
+            v_to = v_grouped[:].rearrange("q (b g h d t) -> q b g h d t", b=B, g=PASSES, h=H, t=PACK)
+            for b in range(B):
+                for g in range(PASSES):
+                    nc.vector.tensor_copy(out=v_to[:, b, g], in_=v_from[:, b, g])
+            v_codes = consts.tile([P, B * PASSES * H * HD], U32, tag="v_codes_" + which, align_bytes=64)
+            v_scales = consts.tile([P, B * PASSES * H * HD], U8, tag="v_scales_" + which, align_bytes=64)
+            nc.vector.quantize_mx(out=v_codes[:].bitcast(FP8X4), scales=v_scales[:], in_=v_grouped[:])
+            return v_codes, v_scales
+
+        heads = [
+            {"b": i // H, "h": i % H, "u": [], "ut": [], "rows": [], "planes": [], "grouped": [], "pt": [],
+             "dt_ps": [], "d_mx": [], "a_mx": []}
+            for i in range(B * H)
+        ]
+
+        def run(x, first, count, step):
+            i, r = divmod(x - first, ROUNDS)
+            if 0 <= i < B * H and r < count:
+                step(heads[i], r)
+
+        with tc.manual_schedule():
+            v_tiles = quantise_values(
+                "tiles", v_d.rearrange("b h (g t q) d -> q (b h g t) d", g=PASSES, t=PACK, q=P)
+            )
+            v_pairs = quantise_values(
+                "pairs", v_d.rearrange("b h (g u q e) d -> q (b h g u) (e d)", g=PASSES, u=2, q=P, e=2)
+            )
+            for x in range((B * H - 1) * ROUNDS + T_A + ROW_TILES + 3):
+                run(x, T_LOAD, 1, load_maps)
+                run(x, T_S - 1, ROW_TILES, spread_factors)
+                run(x, T_S, ROW_TILES, flip_d)
+                run(x, T_S, ROW_TILES, scale_planes)
+                run(x, T_S + 2, ROW_TILES, quantise_s)
+                run(x, T_S + 2, ROW_TILES, lambda head, r: quantise_flipped(head, "d", r))
+                run(x, T_S + 1, ROW_TILES, copy_flipped_d)
+                run(x, T_S + 1, ROW_TILES, regroup)
+                run(x, T_SUMS, ROW_TILES, scale_d)
+                run(x, T_S + 3, ROW_TILES, lambda head, r: times_values(head, "d", r, v_pairs, o_d, out_d))
+                run(x, T_A - 1, ROW_TILES, products)
+                run(x, T_A, ROW_TILES, finish_a)
+                run(x, T_A, ROW_TILES, lambda head, r: quantise_flipped(head, "a", r))
+                run(x, T_SUMS + 2, ROW_TILES, add_r)
+                run(x, T_SUMS + 3, ROW_TILES, flip_sum)
+                run(x, T_A + 2, ROW_TILES, lambda head, r: times_values(head, "a", r, v_tiles, o_rd, out_rd))
+                run(x, T_SUMS + 8, 1, lambda head, r: root_d(head))
+                run(x, T_SUMS + 9, 1, lambda head, r: root_r(head))

@@ -21,17 +21,10 @@ K_PASS = P * PACK
 PASSES = N // K_PASS
 ROW_TILES = N // P
 BANK = 512
-HALVES = N // BANK
 LOAD_TILES = 2
+GROUP_COLS = 512
 CHUNK = 2
-UT_BUFS = PASSES * (ROW_TILES + 2)
-SUM_BUFS = 5
-
-ROUNDS = 2 * ROW_TILES
-T_LOAD = 0
-T_S = T_LOAD + ROUNDS + ROW_TILES
-T_A = T_S + ROW_TILES
-T_SUMS = T_A - ROUNDS - 2
+SUM_BUFS = 2 * ROW_TILES
 
 FLOPS = B * H * (2 * N * N * N + 2 * (2 * N * N * HD))
 
@@ -46,9 +39,9 @@ def tile_multiattention_pa_t_kernel(tc, attn_r, attn_d, v_d, out_rd, out_d):
         consts = ctx.enter_context(tc.tile_pool(name="consts", bufs=1))
         maps = ctx.enter_context(tc.tile_pool(name="maps", bufs=2))
         sums = ctx.enter_context(tc.tile_pool(name="sums", bufs=SUM_BUFS))
-        flipped_sums = ctx.enter_context(tc.tile_pool(name="flipped_sums", bufs=UT_BUFS))
         small = ctx.enter_context(tc.tile_pool(name="small", bufs=2))
-        planes_pool = ctx.enter_context(tc.tile_pool(name="planes", bufs=4))
+        spread = ctx.enter_context(tc.tile_pool(name="spread", bufs=1))
+        planes_pool = ctx.enter_context(tc.tile_pool(name="planes", bufs=2))
         stage = ctx.enter_context(tc.tile_pool(name="stage", bufs=3))
         keep = ctx.enter_context(tc.tile_pool(name="keep", bufs=1))
         outs = ctx.enter_context(tc.tile_pool(name="outs", bufs=1))
@@ -56,8 +49,10 @@ def tile_multiattention_pa_t_kernel(tc, attn_r, attn_d, v_d, out_rd, out_d):
         t_psum = ctx.enter_context(tc.psum_pool(name="t_psum", bufs=2))
         o_psum = ctx.enter_context(tc.psum_pool(name="o_psum", bufs=2))
 
-        ident = consts.tile([P, P], F32)
-        make_identity(nc, ident[:])
+        ident_f32 = consts.tile([P, P], F32)
+        make_identity(nc, ident_f32[:])
+        ident_bf16 = consts.tile([P, P], BF16)
+        make_identity(nc, ident_bf16[:])
         minus_half = consts.tile([P, ROW_TILES], F32)
         nc.vector.memset(minus_half[:], -0.5)
 
@@ -65,14 +60,8 @@ def tile_multiattention_pa_t_kernel(tc, attn_r, attn_d, v_d, out_rd, out_d):
         sr_scales = keep.tile([P, PASSES, N], U8, align_bytes=64)
         sd_codes = keep.tile([P, PASSES, N], U32, align_bytes=64)
         sd_scales = keep.tile([P, PASSES, N], U8, align_bytes=64)
-        s_codes = {"r": sr_codes, "d": sd_codes}
-        s_scales = {"r": sr_scales, "d": sd_scales}
 
-        o_rd = [outs.tile([P, ROW_TILES, H * HD], F32, name="o_rd%d" % b) for b in range(B)]
-        o_d = [outs.tile([P, ROW_TILES, H * HD], F32, name="o_d%d" % b) for b in range(B)]
-
-        def load_maps(head, r):
-            b, h = head["b"], head["h"]
+        def load_maps(b, h):
             w_r = maps.tile([P, ROW_TILES * N], BF16)
             w_d = maps.tile([P, ROW_TILES * N], BF16)
             src_r = attn_r[b, h].rearrange("(r p) j -> p r j", p=P)
@@ -83,9 +72,9 @@ def tile_multiattention_pa_t_kernel(tc, attn_r, attn_d, v_d, out_rd, out_d):
                 nc.sync.dma_start(out=row_tiles(w_r[:])[:, some, :], in_=src_r[:, some, :])
             acc_d = small.tile([P, ROW_TILES], F32)
             acc_u = small.tile([P, ROW_TILES], F32)
-            head["w_r"], head["w_d"], head["acc_d"], head["acc_u"] = w_r, w_d, acc_d, acc_u
+            return {"b": b, "h": h, "w_r": w_r, "w_d": w_d, "acc_d": acc_d, "acc_u": acc_u, "u": []}
 
-        def scale_d(head, r):
+        def add_maps_and_sum_rows(head, r):
             u = sums.tile([P, N], F32)
             nc.scalar.activation(
                 out=u[:],
@@ -94,10 +83,6 @@ def tile_multiattention_pa_t_kernel(tc, attn_r, attn_d, v_d, out_rd, out_d):
                 scale=BETA,
                 accum_out=head["acc_d"][:, r : r + 1],
             )
-            head["u"].append(u)
-
-        def add_r(head, r):
-            u = head["u"][r]
             nc.vector.scalar_tensor_tensor(
                 out=u[:],
                 in0=row_tiles(head["w_r"][:])[:, r, :],
@@ -107,183 +92,161 @@ def tile_multiattention_pa_t_kernel(tc, attn_r, attn_d, v_d, out_rd, out_d):
                 op1=ALU.add,
                 accum_out=head["acc_u"][:, r : r + 1],
             )
+            head["u"].append(u)
 
-        def flip_sum(head, r):
-            u = head["u"][r]
-            for g in range(PASSES):
-                ut_ps = t_psum.tile([P, PACK, P], F32, tag="t_ps")
-                for t in range(PACK):
-                    m0 = g * K_PASS + t * P
-                    nc.tensor.transpose(out=ut_ps[:, t, :], in_=u[:, m0 : m0 + P], identity=ident[:])
-                ut = flipped_sums.tile([P, P, PACK], F32)
-                nc.scalar.copy(out=ut[:], in_=ut_ps[:].rearrange("q t i -> q i t"))
-                head["ut"].append(ut)
+        def spread_along_rows(factor, factor_row):
+            for half in range(N // BANK):
+                row_ps = t_psum.tile([P, BANK // P, P], F32, tag="t_ps")
+                for a in range(BANK // P):
+                    r = half * (BANK // P) + a
+                    nc.tensor.transpose(
+                        out=row_ps[:, a, :],
+                        in_=factor[:, r : r + 1].to_broadcast([P, P]),
+                        identity=ident_f32[:],
+                    )
+                nc.scalar.copy(
+                    out=factor_row[:, half * BANK : (half + 1) * BANK],
+                    in_=row_ps[:].rearrange("p a j -> p (a j)"),
+                )
 
-        def root_d(head):
+        def inverse_roots_of_row_sums(head):
             sum_d = small.tile([P, ROW_TILES], F32)
             nc.vector.tensor_scalar_mul(out=sum_d[:], in0=head["acc_d"][:], scalar1=1.0 / BETA)
             dd = small.tile([P, ROW_TILES], F32)
             nc.gpsimd.tensor_tensor(out=dd[:], in0=sum_d[:], in1=minus_half[:], op=ALU.pow)
-            head["sum_d"], head["d"] = sum_d, dd
+            dd_row = spread.tile([P, N], F32)
+            spread_along_rows(dd, dd_row)
 
-        def root_r(head):
             sum_r = small.tile([P, ROW_TILES], F32)
             nc.vector.scalar_tensor_tensor(
                 out=sum_r[:],
                 in0=head["acc_u"][:],
                 scalar=1.0 / BETA,
-                in1=head["sum_d"][:],
+                in1=sum_d[:],
                 op0=ALU.mult,
                 op1=ALU.subtract,
             )
             dr = small.tile([P, ROW_TILES], F32)
             nc.gpsimd.tensor_tensor(out=dr[:], in0=sum_r[:], in1=minus_half[:], op=ALU.pow)
-            head["r"] = dr
+            dr_row = spread.tile([P, N], F32)
+            spread_along_rows(dr, dr_row)
+            head["dd"], head["dd_row"] = dd, dd_row
+            head["dr"], head["dr_row"] = dr, dr_row
 
-        def piece(j):
-            return "dr"[j // (HALVES * PASSES)], (j // PASSES) % HALVES, j % PASSES
-
-        def spread_factors(head, j):
-            which, half, c = piece(j)
-            if c == 0:
-                row = p_psum.tile([P, BANK // P, P], F32, tag="p_ps")
-                for a in range(BANK // P):
-                    r = half * (BANK // P) + a
-                    nc.tensor.transpose(
-                        out=row[:, a, :],
-                        in_=head[which][:, r : r + 1].to_broadcast([P, P]),
-                        identity=ident[:],
-                    )
-                head["rows"].append(row)
-
-        def scale_planes(head, j):
-            which, half, c = piece(j)
-            cols = slice(half * BANK, (half + 1) * BANK)
-            planes = planes_pool.tile([P, PACK, BANK], BF16)
-            for t in range(PACK):
-                r = PACK * c + t
-                nc.vector.scalar_tensor_tensor(
-                    out=planes[:, t, :],
-                    in0=row_tiles(head["w_" + which][:])[:, r, cols],
-                    scalar=head[which][:, r : r + 1],
-                    in1=head["rows"][j // PASSES][:].rearrange("p a x -> p (a x)"),
-                    op0=ALU.mult,
-                    op1=ALU.mult,
-                )
-            head["planes"].append(planes)
-
-        def regroup(head, j):
-            grouped = stage.tile([P, BANK, PACK], BF16, align_bytes=64)
-            nc.scalar.copy(
-                out=grouped[:].rearrange("p (a i) t -> p a t i", i=4),
-                in_=head["planes"][j][:].rearrange("p t (a i) -> p a t i", i=4),
-            )
-            head["grouped"].append(grouped)
-
-        def quantise_s(head, j):
-            which, half, c = piece(j)
-            cols = slice(half * BANK, (half + 1) * BANK)
-            nc.vector.quantize_mx(
-                out=s_codes[which][:, c, cols].bitcast(FP8X4),
-                scales=s_scales[which][:, c, cols],
-                in_=head["grouped"][j][:].rearrange("p n t -> p (n t)"),
-            )
-
-        def products(head, r):
-            rows = slice(r * P, (r + 1) * P)
-            for g in range(PASSES):
-                pt_ps = p_psum.tile([P, PACK, P], F32, tag="p_ps")
+        def quantise_s(w, factor, factor_row, codes, scales):
+            for c in range(PASSES):
+                planes = planes_pool.tile([P, PACK, N], BF16)
                 for t in range(PACK):
-                    cols = slice(g * K_PASS + t * P, g * K_PASS + (t + 1) * P)
-                    for c in range(PASSES):
-                        nc.tensor.matmul_mx(
-                            out=pt_ps[:, t, :],
-                            lhsT=s_codes["d"][:, c, cols].bitcast(FP8X4),
-                            lhsT_scale=s_scales["d"][:, c, cols],
-                            rhs=s_codes["r"][:, c, rows].bitcast(FP8X4),
-                            rhs_scale=s_scales["r"][:, c, rows],
-                            start=(c == 0),
-                            stop=(c == PASSES - 1),
-                        )
-                head["pt"].append(pt_ps)
+                    r = PACK * c + t
+                    nc.vector.scalar_tensor_tensor(
+                        out=planes[:, t, :],
+                        in0=row_tiles(w[:])[:, r, :],
+                        scalar=factor[:, r : r + 1],
+                        in1=factor_row[:],
+                        op0=ALU.mult,
+                        op1=ALU.mult,
+                    )
+                for n0 in range(0, N, GROUP_COLS):
+                    cols = slice(n0, n0 + GROUP_COLS)
+                    grouped = stage.tile([P, GROUP_COLS, PACK], BF16, align_bytes=64)
+                    nc.scalar.copy(
+                        out=grouped[:].rearrange("p (a i) t -> p a t i", i=4),
+                        in_=planes[:, :, cols].rearrange("p t (a i) -> p a t i", i=4),
+                    )
+                    nc.vector.quantize_mx(
+                        out=codes[:, c, cols].bitcast(FP8X4),
+                        scales=scales[:, c, cols],
+                        in_=grouped[:].rearrange("p n t -> p (n t)"),
+                    )
 
-        def new_flipped(head, key, r):
-            if r % CHUNK == 0:
-                flipped = stage.tile([P, PASSES * CHUNK * P * PACK], BF16, align_bytes=64)
-                head[key] = flipped
-            return head[key], r % CHUNK
-
-        def finish_a(head, r):
-            flipped, slot = new_flipped(head, "a_flipped", r)
-            for g in range(PASSES):
+        def fused_map_rows(head, r):
+            rows = slice(r * P, (r + 1) * P)
+            a_rows = stage.tile([P, N], BF16)
+            for m0 in range(0, N, BANK):
+                cols = slice(m0, m0 + BANK)
+                p_ps = p_psum.tile([P, BANK], F32)
+                for c in range(PASSES):
+                    nc.tensor.matmul_mx(
+                        out=p_ps[:],
+                        lhsT=sr_codes[:, c, rows].bitcast(FP8X4),
+                        lhsT_scale=sr_scales[:, c, rows],
+                        rhs=sd_codes[:, c, cols].bitcast(FP8X4),
+                        rhs_scale=sd_scales[:, c, cols],
+                        start=(c == 0),
+                        stop=(c == PASSES - 1),
+                    )
                 nc.vector.scalar_tensor_tensor(
-                    out=flipped[:].rearrange("q (g i t) -> q g i t", g=PASSES, t=PACK)[
-                        :, g, slot * P : (slot + 1) * P, :
-                    ],
-                    in0=head["pt"][PASSES * r + g][:].rearrange("q t i -> q i t"),
+                    out=a_rows[:, cols],
+                    in0=p_ps[:],
                     scalar=ALPHA,
-                    in1=head["ut"][PASSES * r + g][:],
+                    in1=head["u"][r][:, cols],
                     op0=ALU.mult,
                     op1=ALU.add,
                 )
+            return a_rows
 
-        def flip_d(head, r):
+        def flip_computed_rows(a_rows, flipped, slot):
+            t_ps = t_psum.tile([P, PASSES, PACK, P], BF16, tag="t_ps")
+            for g in range(PASSES):
+                for t in range(PACK):
+                    m0 = g * K_PASS + t * P
+                    nc.tensor.transpose(
+                        out=t_ps[:, g, t, :], in_=a_rows[:, m0 : m0 + P], identity=ident_bf16[:]
+                    )
+            nc.scalar.copy(
+                out=flipped[:].rearrange("q (g i t) -> q g i t", g=PASSES, t=PACK)[
+                    :, :, slot * P : (slot + 1) * P, :
+                ],
+                in_=t_ps[:].rearrange("q g t i -> q g i t"),
+            )
+
+        def flip_input_rows(w, r, flipped, slot):
             t_ps = t_psum.tile([P, PASSES * 2, P], F32, tag="t_ps")
-            words = head["w_d"][:].bitcast(F32).rearrange("i (r x) -> i r x", r=ROW_TILES)
+            words = w[:].bitcast(F32).rearrange("i (r x) -> i r x", r=ROW_TILES)
             for gu in range(PASSES * 2):
                 nc.tensor.transpose(
-                    out=t_ps[:, gu, :], in_=words[:, r, gu * P : (gu + 1) * P], identity=ident[:]
+                    out=t_ps[:, gu, :],
+                    in_=words[:, r, gu * P : (gu + 1) * P],
+                    identity=ident_f32[:],
                 )
-            head["dt_ps"].append(t_ps)
-
-        def copy_flipped_d(head, r):
-            flipped, slot = new_flipped(head, "d_flipped", r)
             nc.scalar.copy(
                 out=flipped[:].bitcast(F32).rearrange("q (g i u) -> q g i u", g=PASSES, u=2)[
                     :, :, slot * P : (slot + 1) * P, :
                 ],
-                in_=head["dt_ps"][r][:].rearrange("q (g u) i -> q g i u", u=2),
+                in_=t_ps[:].rearrange("q (g u) i -> q g i u", u=2),
             )
 
-        def quantise_flipped(head, key, r):
-            if r % CHUNK == CHUNK - 1:
-                f_codes = stage.tile([P, PASSES * CHUNK * P], U32, align_bytes=64)
-                f_scales = stage.tile([P, PASSES * CHUNK * P], U8, align_bytes=64)
-                nc.vector.quantize_mx(
-                    out=f_codes[:].bitcast(FP8X4), scales=f_scales[:], in_=head[key + "_flipped"][:]
-                )
-                head[key + "_mx"].append((f_codes, f_scales))
-
-        def times_values(head, key, r, values, o_sb, out):
-            if r % CHUNK == CHUNK - 1:
-                b, h = head["b"], head["h"]
-                f_codes, f_scales = head[key + "_mx"][r // CHUNK]
-                v_codes, v_scales = values
-                o_ps = o_psum.tile([P, CHUNK, P], F32)
-                for slot in range(CHUNK):
-                    for g in range(PASSES):
-                        rows = slice((g * CHUNK + slot) * P, (g * CHUNK + slot + 1) * P)
-                        vals = slice((b * PASSES + g) * H * HD, (b * PASSES + g + 1) * H * HD)
-                        nc.tensor.matmul_mx(
-                            out=o_ps[:, slot, :],
-                            lhsT=f_codes[:, rows].bitcast(FP8X4),
-                            lhsT_scale=f_scales[:, rows],
-                            rhs=v_codes[:, vals].bitcast(FP8X4),
-                            rhs_scale=v_scales[:, vals],
-                            start=(g == 0),
-                            stop=(g == PASSES - 1),
-                        )
-                mine = slice(h * HD, (h + 1) * HD)
-                some = slice(r + 1 - CHUNK, r + 1)
-                nc.scalar.copy(out=o_sb[b][:, some, mine], in_=o_ps[:, :, mine])
-                if h == H - 1:
-                    nc.sync.dma_start(
-                        out=out[b].rearrange("(r p) c -> p r c", p=P)[:, some, :], in_=o_sb[b][:, some, :]
+        def times_values(flipped, values, head, r0, o_sb, out):
+            b, h = head["b"], head["h"]
+            v_codes, v_scales = values
+            f_codes = stage.tile([P, PASSES * CHUNK * P], U32, align_bytes=64)
+            f_scales = stage.tile([P, PASSES * CHUNK * P], U8, align_bytes=64)
+            nc.vector.quantize_mx(out=f_codes[:].bitcast(FP8X4), scales=f_scales[:], in_=flipped[:])
+            o_ps = o_psum.tile([P, CHUNK, P], F32)
+            for slot in range(CHUNK):
+                for g in range(PASSES):
+                    rows = slice((g * CHUNK + slot) * P, (g * CHUNK + slot + 1) * P)
+                    vals = slice((b * PASSES + g) * H * HD, (b * PASSES + g + 1) * H * HD)
+                    nc.tensor.matmul_mx(
+                        out=o_ps[:, slot, :],
+                        lhsT=f_codes[:, rows].bitcast(FP8X4),
+                        lhsT_scale=f_scales[:, rows],
+                        rhs=v_codes[:, vals].bitcast(FP8X4),
+                        rhs_scale=v_scales[:, vals],
+                        start=(g == 0),
+                        stop=(g == PASSES - 1),
                     )
+            mine = slice(h * HD, (h + 1) * HD)
+            some = slice(r0, r0 + CHUNK)
+            nc.scalar.copy(out=o_sb[:, some, mine], in_=o_ps[:, :, mine])
+            if h == H - 1:
+                nc.sync.dma_start(
+                    out=out[b].rearrange("(r p) c -> p r c", p=P)[:, some, :], in_=o_sb[:, some, :]
+                )
 
         def quantise_values(which, rows_of_v):
             v_rows = stage.tile([P, B * H * N * HD // P], BF16, tag="flipped", align_bytes=64)
-            nc.scalar.dma_start(
+            nc.sync.dma_start(
                 out=v_rows[:].rearrange("q (x y) -> q x y", x=rows_of_v.shape[1]), in_=rows_of_v
             )
             v_grouped = stage.tile([P, B * H * N * HD // P], BF16, tag="flipped", align_bytes=64)
@@ -297,40 +260,48 @@ def tile_multiattention_pa_t_kernel(tc, attn_r, attn_d, v_d, out_rd, out_d):
             nc.vector.quantize_mx(out=v_codes[:].bitcast(FP8X4), scales=v_scales[:], in_=v_grouped[:])
             return v_codes, v_scales
 
-        heads = [
-            {"b": i // H, "h": i % H, "u": [], "ut": [], "rows": [], "planes": [], "grouped": [], "pt": [],
-             "dt_ps": [], "d_mx": [], "a_mx": []}
-            for i in range(B * H)
-        ]
+        heads = [load_maps(0, 0), load_maps(0, 1)]
 
-        def run(x, first, count, step):
-            i, r = divmod(x - first, ROUNDS)
-            if 0 <= i < B * H and r < count:
-                step(heads[i], r)
+        v_tiles = quantise_values(
+            "tiles", v_d.rearrange("b h (g t q) d -> q (b h g t) d", g=PASSES, t=PACK, q=P)
+        )
+        v_pairs = quantise_values(
+            "pairs", v_d.rearrange("b h (g u q e) d -> q (b h g u) (e d)", g=PASSES, u=2, q=P, e=2)
+        )
 
-        with tc.manual_schedule():
-            v_tiles = quantise_values(
-                "tiles", v_d.rearrange("b h (g t q) d -> q (b h g t) d", g=PASSES, t=PACK, q=P)
-            )
-            v_pairs = quantise_values(
-                "pairs", v_d.rearrange("b h (g u q e) d -> q (b h g u) (e d)", g=PASSES, u=2, q=P, e=2)
-            )
-            for x in range((B * H - 1) * ROUNDS + T_A + ROW_TILES + 3):
-                run(x, T_LOAD, 1, load_maps)
-                run(x, T_S - 1, ROW_TILES, spread_factors)
-                run(x, T_S, ROW_TILES, flip_d)
-                run(x, T_S, ROW_TILES, scale_planes)
-                run(x, T_S + 2, ROW_TILES, quantise_s)
-                run(x, T_S + 2, ROW_TILES, lambda head, r: quantise_flipped(head, "d", r))
-                run(x, T_S + 1, ROW_TILES, copy_flipped_d)
-                run(x, T_S + 1, ROW_TILES, regroup)
-                run(x, T_SUMS, ROW_TILES, scale_d)
-                run(x, T_S + 3, ROW_TILES, lambda head, r: times_values(head, "d", r, v_pairs, o_d, out_d))
-                run(x, T_A - 1, ROW_TILES, products)
-                run(x, T_A, ROW_TILES, finish_a)
-                run(x, T_A, ROW_TILES, lambda head, r: quantise_flipped(head, "a", r))
-                run(x, T_SUMS + 2, ROW_TILES, add_r)
-                run(x, T_SUMS + 3, ROW_TILES, flip_sum)
-                run(x, T_A + 2, ROW_TILES, lambda head, r: times_values(head, "a", r, v_tiles, o_rd, out_rd))
-                run(x, T_SUMS + 8, 1, lambda head, r: root_d(head))
-                run(x, T_SUMS + 9, 1, lambda head, r: root_r(head))
+        for r in range(ROW_TILES):
+            add_maps_and_sum_rows(heads[0], r)
+        inverse_roots_of_row_sums(heads[0])
+
+        o_rd = None
+        o_d = None
+        for i in range(B * H):
+            head = heads[i]
+
+            quantise_s(head["w_d"], head["dd"], head["dd_row"], sd_codes, sd_scales)
+            quantise_s(head["w_r"], head["dr"], head["dr_row"], sr_codes, sr_scales)
+
+            if head["h"] == 0:
+                o_rd = outs.tile([P, ROW_TILES, H * HD], F32)
+                o_d = outs.tile([P, ROW_TILES, H * HD], F32)
+
+            for r0 in range(0, ROW_TILES, CHUNK):
+                flipped = stage.tile([P, PASSES * CHUNK * P * PACK], BF16, align_bytes=64)
+                for slot in range(CHUNK):
+                    flip_input_rows(head["w_d"], r0 + slot, flipped, slot)
+                times_values(flipped, v_pairs, head, r0, o_d, out_d)
+
+            if i + 2 < B * H:
+                heads.append(load_maps((i + 2) // H, (i + 2) % H))
+
+            if i + 1 < B * H:
+                for r in range(ROW_TILES):
+                    add_maps_and_sum_rows(heads[i + 1], r)
+                inverse_roots_of_row_sums(heads[i + 1])
+
+            for r0 in range(0, ROW_TILES, CHUNK):
+                flipped = stage.tile([P, PASSES * CHUNK * P * PACK], BF16, align_bytes=64)
+                for slot in range(CHUNK):
+                    a_rows = fused_map_rows(head, r0 + slot)
+                    flip_computed_rows(a_rows, flipped, slot)
+                times_values(flipped, v_tiles, head, r0, o_rd, out_rd)

@@ -22,9 +22,13 @@ PASSES = N // K_PASS
 ROW_TILES = N // P
 BANK = 512
 LOAD_TILES = 2
-GROUP_COLS = 512
+PART = 512
+PARTS = N // PART
 CHUNK = 2
-SUM_BUFS = 2 * ROW_TILES
+CHUNKS = ROW_TILES // CHUNK
+
+TENSOR_ADDS = (0, 6, 4, 4)
+HEAD_SLOTS = 16
 
 FLOPS = B * H * (2 * N * N * N + 2 * (2 * N * N * HD))
 
@@ -33,137 +37,209 @@ def row_tiles(flat):
     return flat.rearrange("p (r j) -> p r j", r=ROW_TILES)
 
 
+def as_words(flat):
+    return flat.bitcast(F32).rearrange("p (r y) -> p r y", r=ROW_TILES)
+
+
 def tile_multiattention_pa_t_kernel(tc, attn_r, attn_d, v_d, out_rd, out_d):
     nc = tc.nc
     with ExitStack() as ctx:
         consts = ctx.enter_context(tc.tile_pool(name="consts", bufs=1))
         maps = ctx.enter_context(tc.tile_pool(name="maps", bufs=2))
-        sums = ctx.enter_context(tc.tile_pool(name="sums", bufs=SUM_BUFS))
+        sums = ctx.enter_context(tc.tile_pool(name="sums", bufs=2 * ROW_TILES - 1))
         small = ctx.enter_context(tc.tile_pool(name="small", bufs=2))
         spread = ctx.enter_context(tc.tile_pool(name="spread", bufs=1))
-        planes_pool = ctx.enter_context(tc.tile_pool(name="planes", bufs=2))
-        stage = ctx.enter_context(tc.tile_pool(name="stage", bufs=3))
+        scaled = ctx.enter_context(tc.tile_pool(name="scaled", bufs=3))
+        grouped = ctx.enter_context(tc.tile_pool(name="grouped", bufs=4))
         keep = ctx.enter_context(tc.tile_pool(name="keep", bufs=1))
+        turned = ctx.enter_context(tc.tile_pool(name="turned", bufs=3))
+        codes = ctx.enter_context(tc.tile_pool(name="codes", bufs=2))
         outs = ctx.enter_context(tc.tile_pool(name="outs", bufs=1))
-        p_psum = ctx.enter_context(tc.psum_pool(name="p_psum", bufs=4))
-        t_psum = ctx.enter_context(tc.psum_pool(name="t_psum", bufs=2))
-        o_psum = ctx.enter_context(tc.psum_pool(name="o_psum", bufs=2))
+        p_psum = ctx.enter_context(tc.psum_pool(name="p_psum", bufs=3))
+        t_psum = ctx.enter_context(tc.psum_pool(name="t_psum", bufs=4))
+        o_psum = ctx.enter_context(tc.psum_pool(name="o_psum", bufs=1))
 
         ident_f32 = consts.tile([P, P], F32)
         make_identity(nc, ident_f32[:])
         ident_bf16 = consts.tile([P, P], BF16)
         make_identity(nc, ident_bf16[:])
-        minus_half = consts.tile([P, ROW_TILES], F32)
-        nc.vector.memset(minus_half[:], -0.5)
+        ones = consts.tile([P, 1], BF16)
+        nc.vector.memset(ones[:], 1.0)
 
         sr_codes = keep.tile([P, PASSES, N], U32, align_bytes=64)
         sr_scales = keep.tile([P, PASSES, N], U8, align_bytes=64)
         sd_codes = keep.tile([P, PASSES, N], U32, align_bytes=64)
         sd_scales = keep.tile([P, PASSES, N], U8, align_bytes=64)
+        s_operand = {"r": (sr_codes, sr_scales), "d": (sd_codes, sd_scales)}
+        v_operand = []
 
-        def load_maps(b, h):
-            w_r = maps.tile([P, ROW_TILES * N], BF16)
-            w_d = maps.tile([P, ROW_TILES * N], BF16)
-            src_r = attn_r[b, h].rearrange("(r p) j -> p r j", p=P)
-            src_d = attn_d[b, h].rearrange("(r p) j -> p r j", p=P)
-            for r0 in range(0, ROW_TILES, LOAD_TILES):
-                some = slice(r0, r0 + LOAD_TILES)
-                nc.sync.dma_start(out=row_tiles(w_d[:])[:, some, :], in_=src_d[:, some, :])
-                nc.sync.dma_start(out=row_tiles(w_r[:])[:, some, :], in_=src_r[:, some, :])
-            acc_d = small.tile([P, ROW_TILES], F32)
-            acc_u = small.tile([P, ROW_TILES], F32)
-            return {"b": b, "h": h, "w_r": w_r, "w_d": w_d, "acc_d": acc_d, "acc_u": acc_u, "u": []}
+        def load(head, which):
+            w = maps.tile([P, ROW_TILES * N], BF16, tag="w_" + which)
+            head["w", which] = w
+            rows = {"r": attn_r, "d": attn_d}[which][head["b"], head["h"]].rearrange("(r p) j -> p r j", p=P)
+            for r in range(0, ROW_TILES, LOAD_TILES):
+                some = slice(r, r + LOAD_TILES)
+                nc.sync.dma_start(out=row_tiles(w[:])[:, some, :], in_=rows[:, some, :])
 
-        def add_maps_and_sum_rows(head, r):
+        def load_both(head):
+            both = []
+            for which in "dr":
+                w = maps.tile([P, ROW_TILES * N], BF16, tag="w_" + which)
+                head["w", which] = w
+                src = {"r": attn_r, "d": attn_d}[which][head["b"], head["h"]]
+                both.append((w, src.rearrange("(r p) j -> p r j", p=P)))
+            for r in range(0, ROW_TILES, LOAD_TILES):
+                some = slice(r, r + LOAD_TILES)
+                for w, rows in both:
+                    nc.sync.dma_start(out=row_tiles(w[:])[:, some, :], in_=rows[:, some, :])
+
+        def quantise_values():
+            v_rows = turned.tile([P, B * H * N * HD // P], BF16, tag="turned_a", align_bytes=64)
+            rows = v_d.rearrange("b h (g u q e) d -> q (b h g u) (e d)", g=PASSES, u=2, q=P, e=2)
+            nc.sync.dma_start(out=v_rows[:].rearrange("q (x y) -> q x y", y=2 * HD), in_=rows)
+            v_grouped = turned.tile([P, B * H * N * HD // P], BF16, tag="turned_a", align_bytes=64)
+            v_from = v_rows[:].rearrange("q (b h g t d) -> q b g h d t", b=B, h=H, g=PASSES, t=PACK)
+            v_to = v_grouped[:].rearrange("q (b g h d t) -> q b g h d t", b=B, g=PASSES, h=H, t=PACK)
+            for b in range(B):
+                for g in range(PASSES):
+                    nc.vector.tensor_copy(out=v_to[:, b, g], in_=v_from[:, b, g])
+            v_codes = consts.tile([P, B * PASSES * H * HD], U32, align_bytes=64)
+            v_scales = consts.tile([P, B * PASSES * H * HD], U8, align_bytes=64)
+            nc.vector.quantize_mx(out=v_codes[:].bitcast(FP8X4), scales=v_scales[:], in_=v_grouped[:])
+            v_operand.extend((v_codes, v_scales))
+
+
+        def scale_wd(head, r):
             u = sums.tile([P, N], F32)
+            head["u", r] = u
             nc.scalar.activation(
                 out=u[:],
-                in_=row_tiles(head["w_d"][:])[:, r, :],
+                in_=row_tiles(head["w", "d"][:])[:, r, :],
                 func=ACT.Copy,
                 scale=BETA,
-                accum_out=head["acc_d"][:, r : r + 1],
+                accum_out=head["sum_d"][:, r : r + 1],
             )
+
+        def add_wr(head, r):
+            u = head["u", r]
             nc.vector.scalar_tensor_tensor(
                 out=u[:],
-                in0=row_tiles(head["w_r"][:])[:, r, :],
+                in0=row_tiles(head["w", "r"][:])[:, r, :],
                 scalar=BETA,
                 in1=u[:],
                 op0=ALU.mult,
                 op1=ALU.add,
-                accum_out=head["acc_u"][:, r : r + 1],
+                accum_out=head["sum_u"][:, 0, r : r + 1],
             )
-            head["u"].append(u)
 
-        def spread_along_rows(factor, factor_row):
+        def add_on_tensor(head, r):
+            u = sums.tile([P, N], F32)
+            head["u", r] = u
+            for half in range(N // BANK):
+                cols = slice(half * BANK, (half + 1) * BANK)
+                u_ps = t_psum.tile([P, BANK], F32, tag="t_ps")
+                for which in "dr":
+                    nc.tensor.matmul(
+                        out=u_ps[:],
+                        lhsT=ident_bf16[:],
+                        rhs=row_tiles(head["w", which][:])[:, r, cols],
+                        start=(which == "d"),
+                        stop=(which == "r"),
+                    )
+                nc.scalar.activation(
+                    out=u[:, cols],
+                    in_=u_ps[:],
+                    func=ACT.Copy,
+                    scale=BETA,
+                    accum_out=head["sum_u"][:, half, r : r + 1],
+                )
+
+        def sum_turned(head, c):
+            sum_ps = o_psum.tile([P, CHUNK], F32, tag="o_ps")
+            values = head["turned", "d", c][:].rearrange("q (g a i t) -> q g a i t", g=PASSES, a=CHUNK, t=PACK)
+            for a in range(CHUNK):
+                for g in range(PASSES):
+                    for t in range(PACK):
+                        nc.tensor.matmul(
+                            out=sum_ps[:, a : a + 1],
+                            lhsT=values[:, g, a, :, t],
+                            rhs=ones[:],
+                            start=(g == 0 and t == 0),
+                            stop=(g == PASSES - 1 and t == PACK - 1),
+                        )
+            nc.scalar.mul(out=head["sum_d"][:, CHUNK * c : CHUNK * (c + 1)], in_=sum_ps[:], mul=BETA)
+
+
+        def roots(head):
+            both = small.tile([P, ROW_TILES], F32)
+            nc.vector.tensor_add(out=both[:], in0=head["sum_u"][:, 0, :], in1=head["sum_u"][:, 1, :])
+            nc.vector.tensor_sub(
+                out=head["sum_d"][:, ROW_TILES:], in0=both[:], in1=head["sum_d"][:, :ROW_TILES]
+            )
+            root = small.tile([P, 2 * ROW_TILES], F32)
+            nc.scalar.activation(out=root[:], in_=head["sum_d"][:], func=ACT.Sqrt, scale=1.0 / BETA)
+            factor = small.tile([P, 2 * ROW_TILES], F32)
+            nc.vector.reciprocal(out=factor[:], in_=root[:])
+            head["factor", "d"] = factor[:, :ROW_TILES]
+            head["factor", "r"] = factor[:, ROW_TILES:]
+
+        def spread_along_rows(head, which):
+            row = spread.tile([P, N], F32, tag="row_" + which)
+            head["row", which] = row
             for half in range(N // BANK):
                 row_ps = t_psum.tile([P, BANK // P, P], F32, tag="t_ps")
                 for a in range(BANK // P):
                     r = half * (BANK // P) + a
                     nc.tensor.transpose(
                         out=row_ps[:, a, :],
-                        in_=factor[:, r : r + 1].to_broadcast([P, P]),
+                        in_=head["factor", which][:, r : r + 1].to_broadcast([P, P]),
                         identity=ident_f32[:],
                     )
                 nc.scalar.copy(
-                    out=factor_row[:, half * BANK : (half + 1) * BANK],
+                    out=row[:, half * BANK : (half + 1) * BANK],
                     in_=row_ps[:].rearrange("p a j -> p (a j)"),
                 )
 
-        def inverse_roots_of_row_sums(head):
-            sum_d = small.tile([P, ROW_TILES], F32)
-            nc.vector.tensor_scalar_mul(out=sum_d[:], in0=head["acc_d"][:], scalar1=1.0 / BETA)
-            dd = small.tile([P, ROW_TILES], F32)
-            nc.gpsimd.tensor_tensor(out=dd[:], in0=sum_d[:], in1=minus_half[:], op=ALU.pow)
-            dd_row = spread.tile([P, N], F32)
-            spread_along_rows(dd, dd_row)
 
-            sum_r = small.tile([P, ROW_TILES], F32)
-            nc.vector.scalar_tensor_tensor(
-                out=sum_r[:],
-                in0=head["acc_u"][:],
-                scalar=1.0 / BETA,
-                in1=sum_d[:],
-                op0=ALU.mult,
-                op1=ALU.subtract,
+        def scale_rows_and_columns(head, which, c):
+            s = scaled.tile([P, PACK, N], BF16)
+            head["s", which, c] = s
+            for t in range(PACK):
+                r = PACK * c + t
+                nc.vector.scalar_tensor_tensor(
+                    out=s[:, t, :],
+                    in0=row_tiles(head["w", which][:])[:, r, :],
+                    scalar=head["factor", which][:, r : r + 1],
+                    in1=head["row", which][:],
+                    op0=ALU.mult,
+                    op1=ALU.mult,
+                )
+
+        def regroup(head, which, c, part):
+            cols = slice(part * PART, (part + 1) * PART)
+            side = grouped.tile([P, PART, PACK], BF16, align_bytes=64)
+            head["side", which, c, part] = side
+            nc.scalar.copy(
+                out=side[:].rearrange("p (a i) t -> p a t i", i=4),
+                in_=head["s", which, c][:, :, cols].rearrange("p t (a i) -> p a t i", i=4),
             )
-            dr = small.tile([P, ROW_TILES], F32)
-            nc.gpsimd.tensor_tensor(out=dr[:], in0=sum_r[:], in1=minus_half[:], op=ALU.pow)
-            dr_row = spread.tile([P, N], F32)
-            spread_along_rows(dr, dr_row)
-            head["dd"], head["dd_row"] = dd, dd_row
-            head["dr"], head["dr_row"] = dr, dr_row
 
-        def quantise_s(w, factor, factor_row, codes, scales):
-            for c in range(PASSES):
-                planes = planes_pool.tile([P, PACK, N], BF16)
-                for t in range(PACK):
-                    r = PACK * c + t
-                    nc.vector.scalar_tensor_tensor(
-                        out=planes[:, t, :],
-                        in0=row_tiles(w[:])[:, r, :],
-                        scalar=factor[:, r : r + 1],
-                        in1=factor_row[:],
-                        op0=ALU.mult,
-                        op1=ALU.mult,
-                    )
-                for n0 in range(0, N, GROUP_COLS):
-                    cols = slice(n0, n0 + GROUP_COLS)
-                    grouped = stage.tile([P, GROUP_COLS, PACK], BF16, align_bytes=64)
-                    nc.scalar.copy(
-                        out=grouped[:].rearrange("p (a i) t -> p a t i", i=4),
-                        in_=planes[:, :, cols].rearrange("p t (a i) -> p a t i", i=4),
-                    )
-                    nc.vector.quantize_mx(
-                        out=codes[:, c, cols].bitcast(FP8X4),
-                        scales=scales[:, c, cols],
-                        in_=grouped[:].rearrange("p n t -> p (n t)"),
-                    )
+        def quantise_s(head, which, c, part):
+            cols = slice(part * PART, (part + 1) * PART)
+            s_codes, s_scales = s_operand[which]
+            nc.vector.quantize_mx(
+                out=s_codes[:, c, cols].bitcast(FP8X4),
+                scales=s_scales[:, c, cols],
+                in_=head["side", which, c, part][:].rearrange("p n t -> p (n t)"),
+            )
 
-        def fused_map_rows(head, r):
+
+        def make_a(head, r):
             rows = slice(r * P, (r + 1) * P)
-            a_rows = stage.tile([P, N], BF16)
-            for m0 in range(0, N, BANK):
-                cols = slice(m0, m0 + BANK)
+            a_rows = turned.tile([P, N], BF16)
+            head["a", r] = a_rows
+            for half in range(N // BANK):
+                cols = slice(half * BANK, (half + 1) * BANK)
                 p_ps = p_psum.tile([P, BANK], F32)
                 for c in range(PASSES):
                     nc.tensor.matmul_mx(
@@ -179,129 +255,140 @@ def tile_multiattention_pa_t_kernel(tc, attn_r, attn_d, v_d, out_rd, out_d):
                     out=a_rows[:, cols],
                     in0=p_ps[:],
                     scalar=ALPHA,
-                    in1=head["u"][r][:, cols],
+                    in1=head["u", r][:, cols],
                     op0=ALU.mult,
                     op1=ALU.add,
                 )
-            return a_rows
 
-        def flip_computed_rows(a_rows, flipped, slot):
-            t_ps = t_psum.tile([P, PASSES, PACK, P], BF16, tag="t_ps")
-            for g in range(PASSES):
-                for t in range(PACK):
-                    m0 = g * K_PASS + t * P
-                    nc.tensor.transpose(
-                        out=t_ps[:, g, t, :], in_=a_rows[:, m0 : m0 + P], identity=ident_bf16[:]
-                    )
-            nc.scalar.copy(
-                out=flipped[:].rearrange("q (g i t) -> q g i t", g=PASSES, t=PACK)[
-                    :, :, slot * P : (slot + 1) * P, :
-                ],
-                in_=t_ps[:].rearrange("q g t i -> q g i t"),
-            )
 
-        def flip_input_rows(w, r, flipped, slot):
+        def turn(head, what, r):
+            words = head["a", r][:].bitcast(F32) if what == "a" else as_words(head["w", "d"][:])[:, r, :]
+            a = r % CHUNK
+            if a == 0:
+                values = turned.tile([P, PASSES * CHUNK * P * PACK], BF16, tag="turned_" + what, align_bytes=64)
+                head["turned", what, r // CHUNK] = values
+            values = head["turned", what, r // CHUNK]
             t_ps = t_psum.tile([P, PASSES * 2, P], F32, tag="t_ps")
-            words = w[:].bitcast(F32).rearrange("i (r x) -> i r x", r=ROW_TILES)
             for gu in range(PASSES * 2):
                 nc.tensor.transpose(
-                    out=t_ps[:, gu, :],
-                    in_=words[:, r, gu * P : (gu + 1) * P],
-                    identity=ident_f32[:],
+                    out=t_ps[:, gu, :], in_=words[:, gu * P : (gu + 1) * P], identity=ident_f32[:]
                 )
             nc.scalar.copy(
-                out=flipped[:].bitcast(F32).rearrange("q (g i u) -> q g i u", g=PASSES, u=2)[
-                    :, :, slot * P : (slot + 1) * P, :
+                out=values[:].bitcast(F32).rearrange("q (g i u) -> q g i u", g=PASSES, u=2)[
+                    :, :, a * P : (a + 1) * P, :
                 ],
                 in_=t_ps[:].rearrange("q (g u) i -> q g i u", u=2),
             )
 
-        def times_values(flipped, values, head, r0, o_sb, out):
-            b, h = head["b"], head["h"]
-            v_codes, v_scales = values
-            f_codes = stage.tile([P, PASSES * CHUNK * P], U32, align_bytes=64)
-            f_scales = stage.tile([P, PASSES * CHUNK * P], U8, align_bytes=64)
-            nc.vector.quantize_mx(out=f_codes[:].bitcast(FP8X4), scales=f_scales[:], in_=flipped[:])
-            o_ps = o_psum.tile([P, CHUNK, P], F32)
-            for slot in range(CHUNK):
+        def quantise_turned(head, what, c):
+            x_codes = codes.tile([P, PASSES * CHUNK * P], U32, align_bytes=64)
+            x_scales = codes.tile([P, PASSES * CHUNK * P], U8, align_bytes=64)
+            head["x", what, c] = x_codes, x_scales
+            nc.vector.quantize_mx(
+                out=x_codes[:].bitcast(FP8X4), scales=x_scales[:], in_=head["turned", what, c][:]
+            )
+
+        def times_values(head, what, c):
+            b = head["b"]
+            x_codes, x_scales = head["x", what, c]
+            v_codes, v_scales = v_operand
+            o_ps = o_psum.tile([P, CHUNK, P], F32, tag="o_ps")
+            head["o_ps", what, c] = o_ps
+            for a in range(CHUNK):
                 for g in range(PASSES):
-                    rows = slice((g * CHUNK + slot) * P, (g * CHUNK + slot + 1) * P)
+                    rows = slice((g * CHUNK + a) * P, (g * CHUNK + a + 1) * P)
                     vals = slice((b * PASSES + g) * H * HD, (b * PASSES + g + 1) * H * HD)
                     nc.tensor.matmul_mx(
-                        out=o_ps[:, slot, :],
-                        lhsT=f_codes[:, rows].bitcast(FP8X4),
-                        lhsT_scale=f_scales[:, rows],
+                        out=o_ps[:, a, :],
+                        lhsT=x_codes[:, rows].bitcast(FP8X4),
+                        lhsT_scale=x_scales[:, rows],
                         rhs=v_codes[:, vals].bitcast(FP8X4),
                         rhs_scale=v_scales[:, vals],
                         start=(g == 0),
                         stop=(g == PASSES - 1),
                     )
+
+        def new_outputs(heads_of_b, what):
+            o_sb = outs.tile([P, ROW_TILES, H * HD], F32, tag="o_" + what)
+            for head in heads_of_b:
+                head["o_sb", what] = o_sb
+
+        def keep_product(head, what, c):
+            b, h = head["b"], head["h"]
             mine = slice(h * HD, (h + 1) * HD)
-            some = slice(r0, r0 + CHUNK)
-            nc.scalar.copy(out=o_sb[:, some, mine], in_=o_ps[:, :, mine])
+            some = slice(c * CHUNK, (c + 1) * CHUNK)
+            o_sb = head["o_sb", what]
+            nc.scalar.copy(out=o_sb[:, some, mine], in_=head["o_ps", what, c][:, :, mine])
             if h == H - 1:
+                out = out_rd if what == "a" else out_d
                 nc.sync.dma_start(
                     out=out[b].rearrange("(r p) c -> p r c", p=P)[:, some, :], in_=o_sb[:, some, :]
                 )
 
-        def quantise_values(which, rows_of_v):
-            v_rows = stage.tile([P, B * H * N * HD // P], BF16, tag="flipped", align_bytes=64)
-            nc.sync.dma_start(
-                out=v_rows[:].rearrange("q (x y) -> q x y", x=rows_of_v.shape[1]), in_=rows_of_v
-            )
-            v_grouped = stage.tile([P, B * H * N * HD // P], BF16, tag="flipped", align_bytes=64)
-            v_from = v_rows[:].rearrange("q (b h g t d) -> q b g h d t", b=B, h=H, g=PASSES, t=PACK)
-            v_to = v_grouped[:].rearrange("q (b g h d t) -> q b g h d t", b=B, g=PASSES, h=H, t=PACK)
-            for b in range(B):
-                for g in range(PASSES):
-                    nc.vector.tensor_copy(out=v_to[:, b, g], in_=v_from[:, b, g])
-            v_codes = consts.tile([P, B * PASSES * H * HD], U32, tag="v_codes_" + which, align_bytes=64)
-            v_scales = consts.tile([P, B * PASSES * H * HD], U8, tag="v_scales_" + which, align_bytes=64)
-            nc.vector.quantize_mx(out=v_codes[:].bitcast(FP8X4), scales=v_scales[:], in_=v_grouped[:])
-            return v_codes, v_scales
 
-        heads = [load_maps(0, 0), load_maps(0, 1)]
+        steps = []
 
-        v_tiles = quantise_values(
-            "tiles", v_d.rearrange("b h (g t q) d -> q (b h g t) d", g=PASSES, t=PACK, q=P)
-        )
-        v_pairs = quantise_values(
-            "pairs", v_d.rearrange("b h (g u q e) d -> q (b h g u) (e d)", g=PASSES, u=2, q=P, e=2)
-        )
+        def at(slot, step, *args):
+            steps.append((slot, step, args))
 
-        for r in range(ROW_TILES):
-            add_maps_and_sum_rows(heads[0], r)
-        inverse_roots_of_row_sums(heads[0])
-
-        o_rd = None
-        o_d = None
+        heads = []
         for i in range(B * H):
-            head = heads[i]
+            sum_d = consts.tile([P, 2 * ROW_TILES], F32, tag="sum_d" + str(i))
+            sum_u = consts.tile([P, 2, ROW_TILES], F32, tag="sum_u" + str(i))
+            nc.gpsimd.memset(sum_u[:], 0.0)
+            heads.append({"b": i // H, "h": i % H, "sum_d": sum_d, "sum_u": sum_u})
 
-            quantise_s(head["w_d"], head["dd"], head["dd_row"], sd_codes, sd_scales)
-            quantise_s(head["w_r"], head["dr"], head["dr_row"], sr_codes, sr_scales)
+        at(-20, quantise_values)
+        at(-20, load_both, heads[0])
+        at(-20, load_both, heads[1])
 
+        for i, head in enumerate(heads):
+            t = HEAD_SLOTS * i
+            first = i == 0
+            for c in range(PASSES):
+                at(t + 2 * c, scale_rows_and_columns, head, "d", c)
+                at(t + 4 + 2 * c, scale_rows_and_columns, head, "r", c)
+                for part in range(PARTS):
+                    for which, slot in (("d", t + 3 + 2 * c + part), ("r", t + 8 + 2 * part + c)):
+                        at(slot, regroup, head, which, c, part)
+                        at(slot + 1.5, quantise_s, head, which, c, part)
             if head["h"] == 0:
-                o_rd = outs.tile([P, ROW_TILES, H * HD], F32)
-                o_d = outs.tile([P, ROW_TILES, H * HD], F32)
-
-            for r0 in range(0, ROW_TILES, CHUNK):
-                flipped = stage.tile([P, PASSES * CHUNK * P * PACK], BF16, align_bytes=64)
-                for slot in range(CHUNK):
-                    flip_input_rows(head["w_d"], r0 + slot, flipped, slot)
-                times_values(flipped, v_pairs, head, r0, o_d, out_d)
-
+                at(t + 6, new_outputs, heads[i : i + H], "a")
+            for r in range(ROW_TILES):
+                at(t + 11 + 0.5 * r, make_a, head, r)
+                at(t + 12 + 0.5 * r, turn, head, "a", r)
+            for c in range(CHUNKS):
+                last = t + 11.5 + c
+                at(last + 3, quantise_turned, head, "a", c)
+                at(last + 4.5, times_values, head, "a", c)
+                at(last + 5, keep_product, head, "a", c)
+            from_d = -10 if first else t - 9
+            if head["h"] == 0:
+                at(from_d - 0.25, new_outputs, heads[i : i + H], "d")
+            for r in range(ROW_TILES):
+                at(from_d + 0.75 * r, turn, head, "d", r)
+            for c in range(CHUNKS):
+                last = from_d + 0.75 * (CHUNK * c + 1)
+                if CHUNK * c < TENSOR_ADDS[i]:
+                    at(last + 1, sum_turned, head, c)
+                at(last + 1.5, quantise_turned, head, "d", c)
+                at(last + 3, times_values, head, "d", c)
+                at(last + 3.5, keep_product, head, "d", c)
+            from_u = -15 if first else t - 10
+            for r in range(ROW_TILES):
+                slot = from_u + 0.75 * r
+                if r < TENSOR_ADDS[i]:
+                    at(slot, add_on_tensor, head, r)
+                else:
+                    at(slot, scale_wd, head, r)
+                    at(slot + 1, add_wr, head, r)
+            last = from_u + 0.75 * (ROW_TILES - 1)
+            at(last + 1.5, roots, head)
+            at(last + 2.5, spread_along_rows, head, "d")
+            at(last + 3, spread_along_rows, head, "r")
             if i + 2 < B * H:
-                heads.append(load_maps((i + 2) // H, (i + 2) % H))
+                at(t + 3.5, load, heads[i + 2], "d")
+                at(t + 7.5, load, heads[i + 2], "r")
 
-            if i + 1 < B * H:
-                for r in range(ROW_TILES):
-                    add_maps_and_sum_rows(heads[i + 1], r)
-                inverse_roots_of_row_sums(heads[i + 1])
-
-            for r0 in range(0, ROW_TILES, CHUNK):
-                flipped = stage.tile([P, PASSES * CHUNK * P * PACK], BF16, align_bytes=64)
-                for slot in range(CHUNK):
-                    a_rows = fused_map_rows(head, r0 + slot)
-                    flip_computed_rows(a_rows, flipped, slot)
-                times_values(flipped, v_tiles, head, r0, o_rd, out_rd)
+        for slot, step, args in sorted(steps, key=lambda entry: entry[0]):
+            step(*args)

@@ -349,16 +349,16 @@ def tile_multiattention_pa_t_kernel(tc, attn_r, attn_d, v_d, out_rd, out_d):
                 at(t + 2 * c, scale_rows_and_columns, head, "d", c)
                 at(t + 4 + 2 * c, scale_rows_and_columns, head, "r", c)
                 for part in range(PARTS):
-                    for which, slot in (("d", t + 3 + 2 * c + part), ("r", t + 8 + 2 * part + c)):
+                    for which, slot in (("d", t + 2.75 + 2 * c + part), ("r", t + 7.75 + 2 * part + c)):
                         at(slot, regroup, head, which, c, part)
                         at(slot + 1.5, quantise_s, head, which, c, part)
             if head["h"] == 0:
                 at(t + 6, new_outputs, heads[i : i + H], "a")
             for r in range(ROW_TILES):
-                at(t + 11 + 0.5 * r, make_a, head, r)
-                at(t + 12 + 0.5 * r, turn, head, "a", r)
+                at(t + 10.5 + 0.6 * r, make_a, head, r)
+                at(t + 11.5 + 0.6 * r, turn, head, "a", r)
             for c in range(CHUNKS):
-                last = t + 11.5 + c
+                last = t + 10.5 + 0.6 * (CHUNK * c + 1)
                 at(last + 3, quantise_turned, head, "a", c)
                 at(last + 4.5, times_values, head, "a", c)
                 at(last + 5, keep_product, head, "a", c)
@@ -366,26 +366,26 @@ def tile_multiattention_pa_t_kernel(tc, attn_r, attn_d, v_d, out_rd, out_d):
             if head["h"] == 0:
                 at(from_d - 0.25, new_outputs, heads[i : i + H], "d")
             for r in range(ROW_TILES):
-                at(from_d + 0.75 * r, turn, head, "d", r)
+                at(from_d + 0.8 * r, turn, head, "d", r)
             for c in range(CHUNKS):
-                last = from_d + 0.75 * (CHUNK * c + 1)
+                last = from_d + 0.8 * (CHUNK * c + 1)
                 if CHUNK * c < TENSOR_ADDS[i]:
                     at(last + 1, sum_turned, head, c)
                 at(last + 1.5, quantise_turned, head, "d", c)
                 at(last + 3, times_values, head, "d", c)
                 at(last + 3.5, keep_product, head, "d", c)
-            from_u = -15 if first else t - 10
+            from_u = -15 if first else t - 9.5
             for r in range(ROW_TILES):
-                slot = from_u + 0.75 * r
+                slot = from_u + 0.8 * r
                 if r < TENSOR_ADDS[i]:
                     at(slot, add_on_tensor, head, r)
                 else:
                     at(slot, scale_wd, head, r)
                     at(slot + 1, add_wr, head, r)
-            last = from_u + 0.75 * (ROW_TILES - 1)
+            last = from_u + 0.8 * (ROW_TILES - 1)
             at(last + 1.5, roots, head)
-            at(last + 2.5, spread_along_rows, head, "d")
-            at(last + 3, spread_along_rows, head, "r")
+            at(t - 1, spread_along_rows, head, "d")
+            at(t - 0.5, spread_along_rows, head, "r")
             if i + 2 < B * H:
                 at(t + 3.5, load, heads[i + 2], "d")
                 at(t + 7.5, load, heads[i + 2], "r")

@@ -88,8 +88,9 @@ def tile_multiattention_pa_t_kernel(tc, attn_r, attn_d, v_d, out_rd, out_d):
                 head["w", which] = w
                 src = {"r": attn_r, "d": attn_d}[which][head["b"], head["h"]]
                 both.append((w, src.rearrange("(r p) j -> p r j", p=P)))
-            for r in range(0, ROW_TILES, LOAD_TILES):
-                some = slice(r, r + LOAD_TILES)
+            tiles = 1 if head is heads[0] else LOAD_TILES
+            for r in range(0, ROW_TILES, tiles):
+                some = slice(r, r + tiles)
                 for w, rows in both:
                     nc.sync.dma_start(out=row_tiles(w[:])[:, some, :], in_=rows[:, some, :])
 

from contextlib import ExitStack

import concourse.mybir as mybir
from concourse.masks import make_identity

F32 = mybir.dt.float32
BF16 = mybir.dt.bfloat16
U32 = mybir.dt.uint32
U8 = mybir.dt.uint8
FP8X4 = mybir.dt.float8_e4m3fn_x4
ALU = mybir.AluOpType
ACT = mybir.ActivationFunctionType

B, H, N, HD = 2, 2, 1024, 64
ALPHA = 0.6
BETA = 1.0 - ALPHA

P = 128
PACK = 4
K_PASS = P * PACK
PASSES = N // K_PASS
ROW_TILES = N // P
BANK = 512
LOAD_TILES = 2
PART = 512
PARTS = N // PART
CHUNK = 2
CHUNKS = ROW_TILES // CHUNK

TENSOR_ADDS = (0, 6, 4, 4)
HEAD_SLOTS = 16

FLOPS = B * H * (2 * N * N * N + 2 * (2 * N * N * HD))


def row_tiles(flat):
    return flat.rearrange("p (r j) -> p r j", r=ROW_TILES)


def as_words(flat):
    return flat.bitcast(F32).rearrange("p (r y) -> p r y", r=ROW_TILES)


def tile_multiattention_pa_t_kernel(tc, attn_r, attn_d, v_d, out_rd, out_d):
    nc = tc.nc
    with ExitStack() as ctx:
        consts = ctx.enter_context(tc.tile_pool(name="consts", bufs=1))
        maps = ctx.enter_context(tc.tile_pool(name="maps", bufs=2))
        sums = ctx.enter_context(tc.tile_pool(name="sums", bufs=2 * ROW_TILES - 1))
        small = ctx.enter_context(tc.tile_pool(name="small", bufs=2))
        spread = ctx.enter_context(tc.tile_pool(name="spread", bufs=1))
        scaled = ctx.enter_context(tc.tile_pool(name="scaled", bufs=3))
        grouped = ctx.enter_context(tc.tile_pool(name="grouped", bufs=4))
        keep = ctx.enter_context(tc.tile_pool(name="keep", bufs=1))
        turned = ctx.enter_context(tc.tile_pool(name="turned", bufs=3))
        codes = ctx.enter_context(tc.tile_pool(name="codes", bufs=2))
        outs = ctx.enter_context(tc.tile_pool(name="outs", bufs=1))
        p_psum = ctx.enter_context(tc.psum_pool(name="p_psum", bufs=3))
        t_psum = ctx.enter_context(tc.psum_pool(name="t_psum", bufs=4))
        o_psum = ctx.enter_context(tc.psum_pool(name="o_psum", bufs=1))

        ident_f32 = consts.tile([P, P], F32)
        make_identity(nc, ident_f32[:])
        ident_bf16 = consts.tile([P, P], BF16)
        make_identity(nc, ident_bf16[:])
        ones = consts.tile([P, 1], BF16)
        nc.vector.memset(ones[:], 1.0)

        sr_codes = keep.tile([P, PASSES, N], U32, align_bytes=64)
        sr_scales = keep.tile([P, PASSES, N], U8, align_bytes=64)
        sd_codes = keep.tile([P, PASSES, N], U32, align_bytes=64)
        sd_scales = keep.tile([P, PASSES, N], U8, align_bytes=64)
        s_operand = {"r": (sr_codes, sr_scales), "d": (sd_codes, sd_scales)}
        v_operand = []

        def load(head, which):
            w = maps.tile([P, ROW_TILES * N], BF16, tag="w_" + which)
            head["w", which] = w
            rows = {"r": attn_r, "d": attn_d}[which][head["b"], head["h"]].rearrange("(r p) j -> p r j", p=P)
            for r in range(0, ROW_TILES, LOAD_TILES):
                some = slice(r, r + LOAD_TILES)
                nc.sync.dma_start(out=row_tiles(w[:])[:, some, :], in_=rows[:, some, :])

        def load_both(head):
            both = []
            for which in "dr":
                w = maps.tile([P, ROW_TILES * N], BF16, tag="w_" + which)
                head["w", which] = w
                src = {"r": attn_r, "d": attn_d}[which][head["b"], head["h"]]
                both.append((w, src.rearrange("(r p) j -> p r j", p=P)))
            tiles = 1 if head is heads[0] else LOAD_TILES
            for r in range(0, ROW_TILES, tiles):
                some = slice(r, r + tiles)
                for w, rows in both:
                    nc.sync.dma_start(out=row_tiles(w[:])[:, some, :], in_=rows[:, some, :])

        def quantise_values():
            v_rows = turned.tile([P, B * H * N * HD // P], BF16, tag="turned_a", align_bytes=64)
            rows = v_d.rearrange("b h (g u q e) d -> q (b h g u) (e d)", g=PASSES, u=2, q=P, e=2)
            nc.sync.dma_start(out=v_rows[:].rearrange("q (x y) -> q x y", y=2 * HD), in_=rows)
            v_grouped = turned.tile([P, B * H * N * HD // P], BF16, tag="turned_a", align_bytes=64)
            v_from = v_rows[:].rearrange("q (b h g t d) -> q b g h d t", b=B, h=H, g=PASSES, t=PACK)
            v_to = v_grouped[:].rearrange("q (b g h d t) -> q b g h d t", b=B, g=PASSES, h=H, t=PACK)
            for b in range(B):
                for g in range(PASSES):
                    nc.vector.tensor_copy(out=v_to[:, b, g], in_=v_from[:, b, g])
            v_codes = consts.tile([P, B * PASSES * H * HD], U32, align_bytes=64)
            v_scales = consts.tile([P, B * PASSES * H * HD], U8, align_bytes=64)
            nc.vector.quantize_mx(out=v_codes[:].bitcast(FP8X4), scales=v_scales[:], in_=v_grouped[:])
            v_operand.extend((v_codes, v_scales))


        def scale_wd(head, r):
            u = sums.tile([P, N], F32)
            head["u", r] = u
            nc.scalar.activation(
                out=u[:],
                in_=row_tiles(head["w", "d"][:])[:, r, :],
                func=ACT.Copy,
                scale=BETA,
                accum_out=head["sum_d"][:, r : r + 1],
            )

        def add_wr(head, r):
            u = head["u", r]
            nc.vector.scalar_tensor_tensor(
                out=u[:],
                in0=row_tiles(head["w", "r"][:])[:, r, :],
                scalar=BETA,
                in1=u[:],
                op0=ALU.mult,
                op1=ALU.add,
                accum_out=head["sum_u"][:, 0, r : r + 1],
            )

        def add_on_tensor(head, r):
            u = sums.tile([P, N], F32)
            head["u", r] = u
            for half in range(N // BANK):
                cols = slice(half * BANK, (half + 1) * BANK)
                u_ps = t_psum.tile([P, BANK], F32, tag="t_ps")
                for which in "dr":
                    nc.tensor.matmul(
                        out=u_ps[:],
                        lhsT=ident_bf16[:],
                        rhs=row_tiles(head["w", which][:])[:, r, cols],
                        start=(which == "d"),
                        stop=(which == "r"),
                    )
                nc.scalar.activation(
                    out=u[:, cols],
                    in_=u_ps[:],
                    func=ACT.Copy,
                    scale=BETA,
                    accum_out=head["sum_u"][:, half, r : r + 1],
                )

        def sum_turned(head, c):
            sum_ps = o_psum.tile([P, CHUNK], F32, tag="o_ps")
            values = head["turned", "d", c][:].rearrange("q (g a i t) -> q g a i t", g=PASSES, a=CHUNK, t=PACK)
            for a in range(CHUNK):
                for g in range(PASSES):
                    for t in range(PACK):
                        nc.tensor.matmul(
                            out=sum_ps[:, a : a + 1],
                            lhsT=values[:, g, a, :, t],
                            rhs=ones[:],
                            start=(g == 0 and t == 0),
                            stop=(g == PASSES - 1 and t == PACK - 1),
                        )
            nc.scalar.mul(out=head["sum_d"][:, CHUNK * c : CHUNK * (c + 1)], in_=sum_ps[:], mul=BETA)


        def roots(head):
            both = small.tile([P, ROW_TILES], F32)
            nc.vector.tensor_add(out=both[:], in0=head["sum_u"][:, 0, :], in1=head["sum_u"][:, 1, :])
            nc.vector.tensor_sub(
                out=head["sum_d"][:, ROW_TILES:], in0=both[:], in1=head["sum_d"][:, :ROW_TILES]
            )
            root = small.tile([P, 2 * ROW_TILES], F32)
            nc.scalar.activation(out=root[:], in_=head["sum_d"][:], func=ACT.Sqrt, scale=1.0 / BETA)
            factor = small.tile([P, 2 * ROW_TILES], F32)
            nc.vector.reciprocal(out=factor[:], in_=root[:])
            head["factor", "d"] = factor[:, :ROW_TILES]
            head["factor", "r"] = factor[:, ROW_TILES:]

        def spread_along_rows(head, which):
            row = spread.tile([P, N], F32, tag="row_" + which)
            head["row", which] = row
            for half in range(N // BANK):
                row_ps = t_psum.tile([P, BANK // P, P], F32, tag="t_ps")
                for a in range(BANK // P):
                    r = half * (BANK // P) + a
                    nc.tensor.transpose(
                        out=row_ps[:, a, :],
                        in_=head["factor", which][:, r : r + 1].to_broadcast([P, P]),
                        identity=ident_f32[:],
                    )
                nc.scalar.copy(
                    out=row[:, half * BANK : (half + 1) * BANK],
                    in_=row_ps[:].rearrange("p a j -> p (a j)"),
                )


        def scale_rows_and_columns(head, which, c):
            s = scaled.tile([P, PACK, N], BF16)
            head["s", which, c] = s
            for t in range(PACK):
                r = PACK * c + t
                nc.vector.scalar_tensor_tensor(
                    out=s[:, t, :],
                    in0=row_tiles(head["w", which][:])[:, r, :],
                    scalar=head["factor", which][:, r : r + 1],
                    in1=head["row", which][:],
                    op0=ALU.mult,
                    op1=ALU.mult,
                )

        def regroup(head, which, c, part):
            cols = slice(part * PART, (part + 1) * PART)
            side = grouped.tile([P, PART, PACK], BF16, align_bytes=64)
            head["side", which, c, part] = side
            nc.scalar.copy(
                out=side[:].rearrange("p (a i) t -> p a t i", i=4),
                in_=head["s", which, c][:, :, cols].rearrange("p t (a i) -> p a t i", i=4),
            )

        def quantise_s(head, which, c, part):
            cols = slice(part * PART, (part + 1) * PART)
            s_codes, s_scales = s_operand[which]
            nc.vector.quantize_mx(
                out=s_codes[:, c, cols].bitcast(FP8X4),
                scales=s_scales[:, c, cols],
                in_=head["side", which, c, part][:].rearrange("p n t -> p (n t)"),
            )


        def make_a(head, r):
            rows = slice(r * P, (r + 1) * P)
            a_rows = turned.tile([P, N], BF16)
            head["a", r] = a_rows
            for half in range(N // BANK):
                cols = slice(half * BANK, (half + 1) * BANK)
                p_ps = p_psum.tile([P, BANK], F32)
                for c in range(PASSES):
                    nc.tensor.matmul_mx(
                        out=p_ps[:],
                        lhsT=sr_codes[:, c, rows].bitcast(FP8X4),
                        lhsT_scale=sr_scales[:, c, rows],
                        rhs=sd_codes[:, c, cols].bitcast(FP8X4),
                        rhs_scale=sd_scales[:, c, cols],
                        start=(c == 0),
                        stop=(c == PASSES - 1),
                    )
                nc.vector.scalar_tensor_tensor(
                    out=a_rows[:, cols],
                    in0=p_ps[:],
                    scalar=ALPHA,
                    in1=head["u", r][:, cols],
                    op0=ALU.mult,
                    op1=ALU.add,
                )


        def turn(head, what, r):
            words = head["a", r][:].bitcast(F32) if what == "a" else as_words(head["w", "d"][:])[:, r, :]
            a = r % CHUNK
            if a == 0:
                values = turned.tile([P, PASSES * CHUNK * P * PACK], BF16, tag="turned_" + what, align_bytes=64)
                head["turned", what, r // CHUNK] = values
            values = head["turned", what, r // CHUNK]
            t_ps = t_psum.tile([P, PASSES * 2, P], F32, tag="t_ps")
            for gu in range(PASSES * 2):
                nc.tensor.transpose(
                    out=t_ps[:, gu, :], in_=words[:, gu * P : (gu + 1) * P], identity=ident_f32[:]
                )
            nc.scalar.copy(
                out=values[:].bitcast(F32).rearrange("q (g i u) -> q g i u", g=PASSES, u=2)[
                    :, :, a * P : (a + 1) * P, :
                ],
                in_=t_ps[:].rearrange("q (g u) i -> q g i u", u=2),
            )

        def quantise_turned(head, what, c):
            x_codes = codes.tile([P, PASSES * CHUNK * P], U32, align_bytes=64)
            x_scales = codes.tile([P, PASSES * CHUNK * P], U8, align_bytes=64)
            head["x", what, c] = x_codes, x_scales
            nc.vector.quantize_mx(
                out=x_codes[:].bitcast(FP8X4), scales=x_scales[:], in_=head["turned", what, c][:]
            )

        def times_values(head, what, c):
            b = head["b"]
            x_codes, x_scales = head["x", what, c]
            v_codes, v_scales = v_operand
            o_ps = o_psum.tile([P, CHUNK, P], F32, tag="o_ps")
            head["o_ps", what, c] = o_ps
            for a in range(CHUNK):
                for g in range(PASSES):
                    rows = slice((g * CHUNK + a) * P, (g * CHUNK + a + 1) * P)
                    vals = slice((b * PASSES + g) * H * HD, (b * PASSES + g + 1) * H * HD)
                    nc.tensor.matmul_mx(
                        out=o_ps[:, a, :],
                        lhsT=x_codes[:, rows].bitcast(FP8X4),
                        lhsT_scale=x_scales[:, rows],
                        rhs=v_codes[:, vals].bitcast(FP8X4),
                        rhs_scale=v_scales[:, vals],
                        start=(g == 0),
                        stop=(g == PASSES - 1),
                    )

        def new_outputs(heads_of_b, what):
            o_sb = outs.tile([P, ROW_TILES, H * HD], F32, tag="o_" + what)
            for head in heads_of_b:
                head["o_sb", what] = o_sb

        def keep_product(head, what, c):
            b, h = head["b"], head["h"]
            mine = slice(h * HD, (h + 1) * HD)
            some = slice(c * CHUNK, (c + 1) * CHUNK)
            o_sb = head["o_sb", what]
            nc.scalar.copy(out=o_sb[:, some, mine], in_=head["o_ps", what, c][:, :, mine])
            if h == H - 1:
                out = out_rd if what == "a" else out_d
                nc.sync.dma_start(
                    out=out[b].rearrange("(r p) c -> p r c", p=P)[:, some, :], in_=o_sb[:, some, :]
                )


        steps = []

        def at(slot, step, *args):
            steps.append((slot, step, args))

        heads = []
        for i in range(B * H):
            sum_d = consts.tile([P, 2 * ROW_TILES], F32, tag="sum_d" + str(i))
            sum_u = consts.tile([P, 2, ROW_TILES], F32, tag="sum_u" + str(i))
            nc.gpsimd.memset(sum_u[:], 0.0)
            heads.append({"b": i // H, "h": i % H, "sum_d": sum_d, "sum_u": sum_u})

        at(-20, quantise_values)
        at(-20, load_both, heads[0])
        at(-20, load_both, heads[1])

        for i, head in enumerate(heads):
            t = HEAD_SLOTS * i
            first = i == 0
            for c in range(PASSES):
                at(t + 2 * c, scale_rows_and_columns, head, "d", c)
                at(t + 4 + 2 * c, scale_rows_and_columns, head, "r", c)
                for part in range(PARTS):
                    for which, slot in (("d", t + 2.75 + 2 * c + part), ("r", t + 7.75 + 2 * part + c)):
                        at(slot, regroup, head, which, c, part)
                        at(slot + 1.5, quantise_s, head, which, c, part)
            if head["h"] == 0:
                at(t + 6, new_outputs, heads[i : i + H], "a")
            for r in range(ROW_TILES):
                at(t + 10.5 + 0.6 * r, make_a, head, r)
                at(t + 11.5 + 0.6 * r, turn, head, "a", r)
            for c in range(CHUNKS):
                last = t + 10.5 + 0.6 * (CHUNK * c + 1)
                at(last + 3, quantise_turned, head, "a", c)
                at(last + 4.5, times_values, head, "a", c)
                at(last + 5, keep_product, head, "a", c)
            from_d = -10 if first else t - 9
            if head["h"] == 0:
                at(from_d - 0.25, new_outputs, heads[i : i + H], "d")
            for r in range(ROW_TILES):
                at(from_d + 0.8 * r, turn, head, "d", r)
            for c in range(CHUNKS):
                last = from_d + 0.8 * (CHUNK * c + 1)
                if CHUNK * c < TENSOR_ADDS[i]:
                    at(last + 1, sum_turned, head, c)
                at(last + 1.5, quantise_turned, head, "d", c)
                at(last + 3, times_values, head, "d", c)
                at(last + 3.5, keep_product, head, "d", c)
            from_u = -15 if first else t - 9.5
            for r in range(ROW_TILES):
                slot = from_u + 0.8 * r
                if r < TENSOR_ADDS[i]:
                    at(slot, add_on_tensor, head, r)
                else:
                    at(slot, scale_wd, head, r)
                    at(slot + 1, add_wr, head, r)
            last = from_u + 0.8 * (ROW_TILES - 1)
            at(last + 1.5, roots, head)
            at(t - 1, spread_along_rows, head, "d")
            at(t - 0.5, spread_along_rows, head, "r")
            if i + 2 < B * H:
                at(t + 3.5, load, heads[i + 2], "d")
                at(t + 7.5, load, heads[i + 2], "r")

        for slot, step, args in sorted(steps, key=lambda entry: entry[0]):
            step(*args)
